import numpy as np
import ml_dtypes


def mxq(x, axis, fmt="e4m3"):
    dtype, down = {"e4m3": (ml_dtypes.float8_e4m3fn, 7), "e5m2": (ml_dtypes.float8_e5m2, 14)}[fmt]
    v = np.moveaxis(np.asarray(x, np.float32).astype(ml_dtypes.bfloat16).astype(np.float64), axis, -1)
    blocks = v.reshape(v.shape[:-1] + (-1, 32))
    amax = np.abs(blocks).max(-1, keepdims=True)
    byte = np.maximum(np.where(amax > 0, np.frexp(amax)[1] - 1 + 127, 0) - down, 1)
    scale = np.exp2(byte - 127.0)
    codes = (blocks / scale).astype(np.float32).astype(dtype).astype(np.float64)
    return np.moveaxis((codes * scale).reshape(v.shape), -1, axis)


WIDE = False


def mx_kscale(k):
    if not WIDE:
        return np.ones(k)
    levels = np.array([10, -10, 5, -5, 0])
    a = np.random.permutation(np.resize(levels, k // 512 * 4)).reshape(k // 512, 4)
    idx = np.arange(k)
    return np.exp2(a[idx // 512, idx % 128 // 32])


BF16 = ml_dtypes.bfloat16


def bf(x):
    return np.asarray(x, np.float32).astype(BF16)


def f64(x):
    return np.asarray(x).astype(np.float64)


E2M1 = np.array([0.0, 0.5, 1.0, 1.5, 2.0, 3.0, 4.0, 6.0, -0.0, -0.5, -1.0, -1.5, -2.0, -3.0, -4.0, -6.0])


def pack_weight(w, fmt):
    k, n = w.shape
    w = f64(bf(w)).reshape(k // 32, 32, n)
    amax = np.abs(w).max(1)
    if fmt == "e4m3":
        byte = np.frexp(amax)[1] - 1 + 127 - 7
    else:
        mant, ex = np.frexp(amax / 6.0)
        byte = np.where(mant > 0.5, ex, ex - 1) + 127
    byte = np.clip(np.where(amax > 0, byte, 1), 1, 254)
    scaled = (w * np.exp2(127.0 - byte)[:, None, :]).reshape(k, n).astype(np.float32)
    by_word = np.ascontiguousarray(scaled.reshape(k // 512, 128, 4, n).transpose(0, 1, 3, 2))
    if fmt == "e4m3":
        words = by_word.astype(ml_dtypes.float8_e4m3fn).view(np.uint8)
    else:
        c = by_word.astype(ml_dtypes.float4_e2m1fn).view(np.uint8) & 0xF
        words = c[..., 0::2] | (c[..., 1::2] << 4)
    return np.ascontiguousarray(words), np.ascontiguousarray(byte.astype(np.uint8).reshape(k // 512, 16, n))


def unpack_weight(words, scales, fmt):
    g, p, n, _ = words.shape
    if fmt == "e4m3":
        vals = np.ascontiguousarray(words).view(ml_dtypes.float8_e4m3fn).astype(np.float64)
    else:
        nib = np.empty((g, p, n, 4), np.uint8)
        nib[..., 0::2] = words & 0xF
        nib[..., 1::2] = words >> 4
        vals = E2M1[nib]
    vals = vals * np.repeat(np.exp2(scales.astype(np.float64) - 127.0), 8, axis=1)[..., None]
    return vals.transpose(0, 1, 3, 2).reshape(g * 512, n)


B, S, D, H, DH, L, R = 2, 512, 2048, 4, 128, 16384, 64
DV = L - L // 2


def setup_inputs():
    u = mx_kscale(DV)
    q_rot = bf(np.random.standard_normal((B, S, H, DH)))
    k_rot = bf(np.random.standard_normal((B, S, H, DH)))
    c_v = bf(np.random.standard_normal((B, S, DV)) * u)
    words, scales = pack_weight(np.random.standard_normal((DV, H * DH)) * 3.0 / np.sqrt(DV) / u[:, None], "e4m3")
    return {"q_rot": q_rot,
            "k_rot": k_rot,
            "c_v": c_v,
            "W_v_dec_words": words,
            "W_v_dec_scales": scales}


def reference(q_rot, k_rot, c_v, W_v_dec_words, W_v_dec_scales):
    v = (mxq(f64(c_v), 2, "e4m3") @ unpack_weight(W_v_dec_words, W_v_dec_scales, "e4m3")).reshape(B, S, H, DH)
    sc = f64(q_rot).transpose(0, 2, 1, 3) @ f64(k_rot).transpose(0, 2, 3, 1) * (1.0 / np.sqrt(DH))
    e = np.exp(sc - sc.max(-1, keepdims=True))
    ctx = (mxq(e, 3, "e4m3") @ mxq(v.transpose(0, 2, 1, 3), 2, "e4m3")) / e.sum(-1, keepdims=True)
    return ctx.transpose(0, 2, 1, 3).reshape(B, S, H * DH)

@@ -1,0 +1,317 @@
+from contextlib import ExitStack
+import math
+
+import concourse.mybir as mybir
+from concourse.masks import make_identity
+
+F32 = mybir.dt.float32
+BF16 = mybir.dt.bfloat16
+I32 = mybir.dt.int32
+U32 = mybir.dt.uint32
+U8 = mybir.dt.uint8
+FP8X4 = mybir.dt.float8_e4m3fn_x4
+
+P = 128
+PACK = 4
+K_PASS = P * PACK
+
+BATCHES = 2
+TOKENS = 512
+HEADS = 4
+HEAD_DIM = 128
+LATENT = 8192
+V_WIDTH = HEADS * HEAD_DIM
+
+PASSES = LATENT // K_PASS
+ROW_TILES = TOKENS // P
+ROUND_PASSES = 8
+ROUNDS_PER_TILE = PASSES // ROUND_PASSES
+ROUNDS_PER_BATCH = ROW_TILES * ROUNDS_PER_TILE
+ROUNDS = BATCHES * ROUNDS_PER_BATCH
+ROUND_K = ROUND_PASSES * K_PASS
+WORDS_PER_PASS = K_PASS // 2
+
+STEP_TILES = 2
+STEPS_PER_HEAD = ROW_TILES // STEP_TILES
+STEPS = BATCHES * HEADS * STEPS_PER_HEAD
+
+CV_LEAD = 2
+ATTENTION_LEAD = 4
+CV_RAW_BUFS = 6
+
+SOFTMAX_SCALE = 1.0 / math.sqrt(HEAD_DIM)
+
+FLOPS = 2 * BATCHES * TOKENS * LATENT * V_WIDTH + 2 * 2 * BATCHES * HEADS * TOKENS * TOKENS * HEAD_DIM
+
+
+def tile_multiheadlatentattention_pb_k_kernel(
+    tc, q_rot, k_rot, c_v, W_v_dec_words, W_v_dec_scales, out
+):
+    nc = tc.nc
+    with ExitStack() as stack:
+        keep = stack.enter_context(tc.tile_pool(name="keep", bufs=1))
+        raw_pool = stack.enter_context(tc.tile_pool(name="raw", bufs=CV_RAW_BUFS))
+        grouped_pool = stack.enter_context(tc.tile_pool(name="grouped", bufs=2))
+        codes_pool = stack.enter_context(tc.tile_pool(name="codes", bufs=CV_LEAD + 1))
+        soft_pool = stack.enter_context(tc.tile_pool(name="soft", bufs=2))
+        small_pool = stack.enter_context(tc.tile_pool(name="small", bufs=3))
+        out_pool = stack.enter_context(tc.tile_pool(name="result", bufs=ROW_TILES))
+        work_psum = stack.enter_context(tc.psum_pool(name="work", bufs=5))
+        score_psum = stack.enter_context(tc.psum_pool(name="score", bufs=STEP_TILES))
+        v_psum = stack.enter_context(tc.psum_pool(name="v", bufs=1))
+        stack.enter_context(tc.manual_schedule())
+
+        ident_f32 = keep.tile([P, P], F32)
+        ident_bf16 = keep.tile([P, P], BF16)
+        w_words = keep.tile([P, PASSES, PACK * V_WIDTH], U8, align_bytes=64)
+        w_scales = keep.tile([P, PASSES, V_WIDTH], U8, align_bytes=64)
+        q_rows = keep.tile([P, BATCHES, ROW_TILES, V_WIDTH], BF16)
+        k_rows = keep.tile([P, BATCHES, ROW_TILES, V_WIDTH], BF16)
+        qk_t = keep.tile([P, BATCHES * HEADS, 2, TOKENS], BF16)
+        e_codes = keep.tile([P, STEPS, STEP_TILES * P], U32, align_bytes=64)
+        e_scales = keep.tile([P, STEPS, STEP_TILES * P], U8, align_bytes=64)
+        row_sums = keep.tile([P, BATCHES * ROW_TILES, HEADS], F32)
+        v_grouped = keep.tile([P, BATCHES, V_WIDTH, PACK], BF16, align_bytes=64)
+        v_codes = keep.tile([P, BATCHES, V_WIDTH], U32, align_bytes=64)
+        v_scales = keep.tile([P, BATCHES, V_WIDTH], U8, align_bytes=64)
+
+        cv_raw_of = {}
+        grouped_of = {}
+        cv_codes_of = {}
+        v_acc_of = {}
+        score_of = {}
+        shift_of = {}
+        e_rows_of = {}
+        e_grouped_of = {}
+
+        cv_tiles = c_v.rearrange("b (u p e) k -> b u e p k", u=2, e=2)
+
+        def load_qk(b):
+            nc.sync.dma_start(out=q_rows[:, b], in_=q_rot[b].rearrange("(i p) h d -> p i (h d)", p=P))
+            nc.sync.dma_start(out=k_rows[:, b], in_=k_rot[b].rearrange("(i p) h d -> p i (h d)", p=P))
+
+        def load_cv(i):
+            if not 0 <= i < ROUNDS:
+                return
+            row_tile, half = divmod(i, ROUNDS_PER_TILE)
+            b, j = divmod(row_tile, ROW_TILES)
+            u, e = divmod(j, 2)
+            cv_raw = raw_pool.tile([P, ROUND_K], BF16)
+            nc.sync.dma_start(out=cv_raw[:], in_=cv_tiles[b, u, e, :, half * ROUND_K : (half + 1) * ROUND_K])
+            cv_raw_of[i] = cv_raw
+
+        def load_w_scales():
+            for quadrant in range(4):
+                nc.sync.dma_start(
+                    out=w_scales[32 * quadrant : 32 * quadrant + 4].bitcast(I32),
+                    in_=W_v_dec_scales[:, 4 * quadrant : 4 * quadrant + 4, :]
+                    .rearrange("g r n -> r g n")
+                    .bitcast(I32),
+                )
+
+        def load_w_words(first_pass, n_passes):
+            passes = slice(first_pass, first_pass + n_passes)
+            nc.sync.dma_start(
+                out=w_words[:, passes, :].bitcast(I32),
+                in_=W_v_dec_words[passes].rearrange("g p n t -> p g (n t)").bitcast(I32),
+            )
+
+        def transpose_cv(i):
+            if not 0 <= i < ROUNDS:
+                return
+            cv_words = cv_raw_of[i][:].bitcast(F32)
+            grouped = grouped_pool.tile([P, ROUND_PASSES, P, PACK], BF16, align_bytes=64)
+            banks = ROUND_PASSES // 2
+            for c in range(banks):
+                bank = work_psum.tile([P, 2, 2, P], F32, tag="work")
+                for g in range(2):
+                    first = (2 * c + g) * WORDS_PER_PASS
+                    for u in range(2):
+                        nc.tensor.transpose(
+                            bank[:, g, u, :], cv_words[:, first + u : first + WORDS_PER_PASS : 2], ident_f32[:]
+                        )
+                copy = nc.vector.tensor_copy if c == banks - 1 else nc.scalar.copy
+                copy(out=grouped[:, 2 * c : 2 * c + 2].bitcast(F32), in_=bank[:].rearrange("p g u t -> p g t u"))
+            grouped_of[i] = grouped
+
+        def quantise_cv(i):
+            if not 0 <= i < ROUNDS:
+                return
+            cv_codes = codes_pool.tile([P, ROUND_PASSES * P], U32, align_bytes=64)
+            cv_scales = codes_pool.tile([P, ROUND_PASSES * P], U8, align_bytes=64)
+            nc.vector.quantize_mx(
+                out=cv_codes[:].bitcast(FP8X4),
+                scales=cv_scales[:],
+                in_=grouped_of[i][:].rearrange("p g t j -> p (g t j)"),
+            )
+            cv_codes_of[i] = (cv_codes, cv_scales)
+
+        def project(i):
+            if not 0 <= i < ROUNDS:
+                return
+            row_tile, half = divmod(i, ROUNDS_PER_TILE)
+            if half == 0:
+                v_acc = v_psum.tile([P, V_WIDTH], F32)
+                v_acc_of[row_tile] = v_acc
+            v_acc = v_acc_of[row_tile]
+            cv_codes, cv_scales = cv_codes_of[i]
+            for g in range(ROUND_PASSES):
+                k_pass = half * ROUND_PASSES + g
+                tokens = slice(g * P, (g + 1) * P)
+                nc.tensor.matmul_mx(
+                    out=v_acc[:],
+                    lhsT=cv_codes[:, tokens].bitcast(FP8X4),
+                    lhsT_scale=cv_scales[:, tokens],
+                    rhs=w_words[:, k_pass, :].bitcast(FP8X4),
+                    rhs_scale=w_scales[:, k_pass, :],
+                    start=(k_pass == 0),
+                    stop=(k_pass == PASSES - 1),
+                )
+            if half < ROUNDS_PER_TILE - 1:
+                return
+            b, j = divmod(row_tile, ROW_TILES)
+            nc.scalar.copy(out=v_grouped[:, b, :, j], in_=v_acc[:])
+            if j == ROW_TILES - 1:
+                nc.vector.quantize_mx(
+                    out=v_codes[:, b, :].bitcast(FP8X4),
+                    scales=v_scales[:, b, :],
+                    in_=v_grouped[:, b].rearrange("p n j -> p (n j)"),
+                )
+
+        def transpose_qk(head_block):
+            if not 0 <= head_block < BATCHES * HEADS:
+                return
+            b, h = divmod(head_block, HEADS)
+            qk_bank = work_psum.tile([P, 2, TOKENS], BF16, tag="work")
+            for side, rows in enumerate((q_rows, k_rows)):
+                for i in range(ROW_TILES):
+                    nc.tensor.transpose(
+                        qk_bank[:, side, i * P : (i + 1) * P], rows[:, b, i, h * P : (h + 1) * P], ident_bf16[:]
+                    )
+            nc.scalar.copy(out=qk_t[:, head_block], in_=qk_bank[:])
+
+        def scores(step):
+            if not 0 <= step < STEPS:
+                return
+            head_block, pair = divmod(step, STEPS_PER_HEAD)
+            peak = small_pool.tile([P, STEP_TILES], F32)
+            for a in range(STEP_TILES):
+                i = pair * STEP_TILES + a
+                score = score_psum.tile([P, TOKENS], F32)
+                nc.tensor.matmul(
+                    out=score[:],
+                    lhsT=qk_t[:, head_block, 0, i * P : (i + 1) * P],
+                    rhs=qk_t[:, head_block, 1, :],
+                    start=True,
+                    stop=True,
+                )
+                nc.vector.tensor_reduce(
+                    out=peak[:, a : a + 1], in_=score[:], axis=mybir.AxisListType.X, op=mybir.AluOpType.max
+                )
+                score_of[(step, a)] = score
+            shift = small_pool.tile([P, STEP_TILES], F32)
+            nc.vector.tensor_scalar_mul(out=shift[:], in0=peak[:], scalar1=-SOFTMAX_SCALE)
+            shift_of[step] = shift
+
+        def exponentials(step):
+            if not 0 <= step < STEPS:
+                return
+            head_block, pair = divmod(step, STEPS_PER_HEAD)
+            b, h = divmod(head_block, HEADS)
+            e_rows = soft_pool.tile([P, STEP_TILES, TOKENS], BF16)
+            for a in range(STEP_TILES):
+                i = pair * STEP_TILES + a
+                nc.scalar.activation(
+                    out=e_rows[:, a, :],
+                    in_=score_of[(step, a)][:],
+                    func=mybir.ActivationFunctionType.Exp,
+                    bias=shift_of[step][:, a : a + 1],
+                    scale=SOFTMAX_SCALE,
+                    accum_out=row_sums[:, b * ROW_TILES + i, h : h + 1],
+                )
+            e_rows_of[step] = e_rows
+
+        def transpose_e(step):
+            if not 0 <= step < STEPS:
+                return
+            e_bank = work_psum.tile([P, STEP_TILES, 2, P], F32, tag="work")
+            for a in range(STEP_TILES):
+                e_words = e_rows_of[step][:, a, :].bitcast(F32)
+                for u in range(2):
+                    nc.tensor.transpose(e_bank[:, a, u, :], e_words[:, u * P : (u + 1) * P], ident_f32[:])
+            e_grouped = soft_pool.tile([P, STEP_TILES, P, PACK], BF16, align_bytes=64)
+            nc.vector.tensor_copy(out=e_grouped[:].bitcast(F32), in_=e_bank[:].rearrange("p a u q -> p a q u"))
+            e_grouped_of[step] = e_grouped
+
+        def quantise_e(step):
+            if not 0 <= step < STEPS:
+                return
+            nc.vector.quantize_mx(
+                out=e_codes[:, step, :].bitcast(FP8X4),
+                scales=e_scales[:, step, :],
+                in_=e_grouped_of[step][:].rearrange("p a q j -> p (a q j)"),
+            )
+
+        def context(b, i):
+            if not (0 <= b < BATCHES and i < ROW_TILES):
+                return
+            pair, a = divmod(i, STEP_TILES)
+            queries = slice(a * P, (a + 1) * P)
+            ctx_bank = work_psum.tile([P, HEADS, HEAD_DIM], F32, tag="work")
+            for h in range(HEADS):
+                step = (b * HEADS + h) * STEPS_PER_HEAD + pair
+                head = slice(h * HEAD_DIM, (h + 1) * HEAD_DIM)
+                nc.tensor.matmul_mx(
+                    out=ctx_bank[:, h, :],
+                    lhsT=e_codes[:, step, queries].bitcast(FP8X4),
+                    lhsT_scale=e_scales[:, step, queries],
+                    rhs=v_codes[:, b, head].bitcast(FP8X4),
+                    rhs_scale=v_scales[:, b, head],
+                    start=True,
+                    stop=True,
+                )
+            inverse = small_pool.tile([P, HEADS], F32)
+            nc.vector.reciprocal(out=inverse[:], in_=row_sums[:, b * ROW_TILES + i, :])
+            ctx_rows = out_pool.tile([P, HEADS, HEAD_DIM], F32)
+            nc.vector.tensor_tensor(
+                out=ctx_rows[:],
+                in0=ctx_bank[:],
+                in1=inverse[:].unsqueeze(2).to_broadcast([P, HEADS, HEAD_DIM]),
+                op=mybir.AluOpType.mult,
+            )
+            nc.sync.dma_start(out=out[b, i * P : (i + 1) * P, :], in_=ctx_rows[:].rearrange("p h d -> p (h d)"))
+
+        nc.vector.memset(w_scales[:].rearrange("p g n -> p (g n)").bitcast(I32), 0)
+        make_identity(nc, ident_bf16[:])
+        make_identity(nc, ident_f32[:])
+        load_qk(0)
+        load_cv(0)
+        load_cv(1)
+        load_cv(2)
+        load_w_scales()
+        load_w_words(0, 4)
+        load_w_words(4, 4)
+        load_cv(3)
+        load_w_words(8, 4)
+        load_w_words(12, 4)
+        load_qk(1)
+        load_cv(4)
+        load_cv(5)
+
+        first_turn = -max(ATTENTION_LEAD + 2, CV_LEAD)
+        for turn in range(first_turn, ROUNDS + ROW_TILES):
+            step = turn + ATTENTION_LEAD
+            freed = turn + CV_LEAD - 1
+            if freed >= 0:
+                load_cv(freed + CV_RAW_BUFS)
+            transpose_e(step)
+            if step % STEPS_PER_HEAD == 0:
+                transpose_qk(step // STEPS_PER_HEAD + 1)
+            scores(step + 1)
+            quantise_e(step)
+            transpose_cv(turn + CV_LEAD)
+            exponentials(step + 1)
+            quantise_cv(turn + CV_LEAD)
+            project(turn)
+            b, i = divmod(turn - ROUNDS_PER_BATCH, ROUNDS_PER_BATCH)
+            context(b, i)

@@ -35,9 +35,9 @@ STEP_TILES = 2
 STEPS_PER_HEAD = ROW_TILES // STEP_TILES
 STEPS = BATCHES * HEADS * STEPS_PER_HEAD
 
-CV_LEAD = 2
-ATTENTION_LEAD = 4
-CV_RAW_BUFS = 6
+CV_LEAD = 3
+ATTENTION_LEAD = 3
+CV_RAW_BUFS = 7
 
 SOFTMAX_SCALE = 1.0 / math.sqrt(HEAD_DIM)
 
@@ -56,9 +56,9 @@ def tile_multiheadlatentattention_pb_k_kernel(
         soft_pool = stack.enter_context(tc.tile_pool(name="soft", bufs=2))
         small_pool = stack.enter_context(tc.tile_pool(name="small", bufs=3))
         out_pool = stack.enter_context(tc.tile_pool(name="result", bufs=ROW_TILES))
-        work_psum = stack.enter_context(tc.psum_pool(name="work", bufs=5))
+        work_psum = stack.enter_context(tc.psum_pool(name="work", bufs=4))
         score_psum = stack.enter_context(tc.psum_pool(name="score", bufs=STEP_TILES))
-        v_psum = stack.enter_context(tc.psum_pool(name="v", bufs=1))
+        v_psum = stack.enter_context(tc.psum_pool(name="v", bufs=2))
         stack.enter_context(tc.manual_schedule())
 
         ident_f32 = keep.tile([P, P], F32)
@@ -71,6 +71,7 @@ def tile_multiheadlatentattention_pb_k_kernel(
         e_codes = keep.tile([P, STEPS, STEP_TILES * P], U32, align_bytes=64)
         e_scales = keep.tile([P, STEPS, STEP_TILES * P], U8, align_bytes=64)
         row_sums = keep.tile([P, BATCHES * ROW_TILES, HEADS], F32)
+        inverse_sums = keep.tile([P, BATCHES * ROW_TILES, HEADS], F32)
         v_grouped = keep.tile([P, BATCHES, V_WIDTH, PACK], BF16, align_bytes=64)
         v_codes = keep.tile([P, BATCHES, V_WIDTH], U32, align_bytes=64)
         v_scales = keep.tile([P, BATCHES, V_WIDTH], U8, align_bytes=64)
@@ -251,6 +252,10 @@ def tile_multiheadlatentattention_pb_k_kernel(
                 scales=e_scales[:, step, :],
                 in_=e_grouped_of[step][:].rearrange("p a q j -> p (a q j)"),
             )
+            b, step_in_batch = divmod(step, STEPS // BATCHES)
+            if step_in_batch == STEPS // BATCHES - 1:
+                tiles = slice(b * ROW_TILES, (b + 1) * ROW_TILES)
+                nc.vector.reciprocal(out=inverse_sums[:, tiles, :], in_=row_sums[:, tiles, :])
 
         def context(b, i):
             if not (0 <= b < BATCHES and i < ROW_TILES):
@@ -270,13 +275,12 @@ def tile_multiheadlatentattention_pb_k_kernel(
                     start=True,
                     stop=True,
                 )
-            inverse = small_pool.tile([P, HEADS], F32)
-            nc.vector.reciprocal(out=inverse[:], in_=row_sums[:, b * ROW_TILES + i, :])
+            inverse = inverse_sums[:, b * ROW_TILES + i, :]
             ctx_rows = out_pool.tile([P, HEADS, HEAD_DIM], F32)
             nc.vector.tensor_tensor(
                 out=ctx_rows[:],
                 in0=ctx_bank[:],
-                in1=inverse[:].unsqueeze(2).to_broadcast([P, HEADS, HEAD_DIM]),
+                in1=inverse.unsqueeze(2).to_broadcast([P, HEADS, HEAD_DIM]),
                 op=mybir.AluOpType.mult,
             )
             nc.sync.dma_start(out=out[b, i * P : (i + 1) * P, :], in_=ctx_rows[:].rearrange("p h d -> p (h d)"))
@@ -285,18 +289,17 @@ def tile_multiheadlatentattention_pb_k_kernel(
         make_identity(nc, ident_bf16[:])
         make_identity(nc, ident_f32[:])
         load_qk(0)
-        load_cv(0)
-        load_cv(1)
-        load_cv(2)
+        for i in range(CV_LEAD + 1):
+            load_cv(i)
         load_w_scales()
         load_w_words(0, 4)
         load_w_words(4, 4)
-        load_cv(3)
+        load_cv(CV_LEAD + 1)
         load_w_words(8, 4)
         load_w_words(12, 4)
+        for i in range(CV_LEAD + 2, CV_RAW_BUFS):
+            load_cv(i)
         load_qk(1)
-        load_cv(4)
-        load_cv(5)
 
         first_turn = -max(ATTENTION_LEAD + 2, CV_LEAD)
         for turn in range(first_turn, ROUNDS + ROW_TILES):
@@ -304,13 +307,13 @@ def tile_multiheadlatentattention_pb_k_kernel(
             freed = turn + CV_LEAD - 1
             if freed >= 0:
                 load_cv(freed + CV_RAW_BUFS)
-            transpose_e(step)
+            transpose_cv(turn + CV_LEAD)
+            scores(step + 1)
             if step % STEPS_PER_HEAD == 0:
                 transpose_qk(step // STEPS_PER_HEAD + 1)
-            scores(step + 1)
-            quantise_e(step)
-            transpose_cv(turn + CV_LEAD)
+            transpose_e(step)
             exponentials(step + 1)
+            quantise_e(step)
             quantise_cv(turn + CV_LEAD)
             project(turn)
             b, i = divmod(turn - ROUNDS_PER_BATCH, ROUNDS_PER_BATCH)

@@ -103,11 +103,11 @@ def tile_multiheadlatentattention_pb_k_kernel(
 
         def load_w_scales():
             for quadrant in range(4):
-                nc.sync.dma_start(
-                    out=w_scales[32 * quadrant : 32 * quadrant + 4].bitcast(I32),
+                nc.gpsimd.dma_start(
+                    out=w_scales[32 * quadrant : 32 * quadrant + 4].bitcast(F32),
                     in_=W_v_dec_scales[:, 4 * quadrant : 4 * quadrant + 4, :]
                     .rearrange("g r n -> r g n")
-                    .bitcast(I32),
+                    .bitcast(F32),
                 )
 
         def load_w_words(first_pass, n_passes):
@@ -288,10 +288,10 @@ def tile_multiheadlatentattention_pb_k_kernel(
         nc.vector.memset(w_scales[:].rearrange("p g n -> p (g n)").bitcast(I32), 0)
         make_identity(nc, ident_bf16[:])
         make_identity(nc, ident_f32[:])
+        load_w_scales()
         load_qk(0)
         for i in range(CV_LEAD + 1):
             load_cv(i)
-        load_w_scales()
         load_w_words(0, 4)
         load_w_words(4, 4)
         load_cv(CV_LEAD + 1)

@@ -72,6 +72,7 @@ def tile_multiheadlatentattention_pb_k_kernel(
         e_scales = keep.tile([P, STEPS, STEP_TILES * P], U8, align_bytes=64)
         row_sums = keep.tile([P, BATCHES * ROW_TILES, HEADS], F32)
         inverse_sums = keep.tile([P, BATCHES * ROW_TILES, HEADS], F32)
+        v_rows = keep.tile([P, BATCHES, ROW_TILES, V_WIDTH], BF16)
         v_grouped = keep.tile([P, BATCHES, V_WIDTH, PACK], BF16, align_bytes=64)
         v_codes = keep.tile([P, BATCHES, V_WIDTH], U32, align_bytes=64)
         v_scales = keep.tile([P, BATCHES, V_WIDTH], U8, align_bytes=64)
@@ -171,8 +172,9 @@ def tile_multiheadlatentattention_pb_k_kernel(
             if half < ROUNDS_PER_TILE - 1:
                 return
             b, j = divmod(row_tile, ROW_TILES)
-            nc.scalar.copy(out=v_grouped[:, b, :, j], in_=v_acc[:])
+            nc.scalar.copy(out=v_rows[:, b, j, :], in_=v_acc[:])
             if j == ROW_TILES - 1:
+                nc.vector.tensor_copy(out=v_grouped[:, b], in_=v_rows[:, b].rearrange("p j n -> p n j"))
                 nc.vector.quantize_mx(
                     out=v_codes[:, b, :].bitcast(FP8X4),
                     scales=v_scales[:, b, :],
@@ -286,6 +288,9 @@ def tile_multiheadlatentattention_pb_k_kernel(
             nc.sync.dma_start(out=out[b, i * P : (i + 1) * P, :], in_=ctx_rows[:].rearrange("p h d -> p (h d)"))
 
         nc.vector.memset(w_scales[:].rearrange("p g n -> p (g n)").bitcast(I32), 0)
+        warm = small_pool.tile([P, 1], F32)
+        nc.vector.memset(warm[:], 0.0)
+        nc.scalar.activation(out=warm[:], in_=warm[:], func=mybir.ActivationFunctionType.Exp)
         make_identity(nc, ident_bf16[:])
         make_identity(nc, ident_f32[:])
         load_w_scales()

@@ -37,7 +37,7 @@ STEPS = BATCHES * HEADS * STEPS_PER_HEAD
 
 CV_LEAD = 3
 ATTENTION_LEAD = 3
-CV_RAW_BUFS = 7
+CV_RAW_BUFS = 5
 
 SOFTMAX_SCALE = 1.0 / math.sqrt(HEAD_DIM)
 
@@ -51,6 +51,7 @@ def tile_multiheadlatentattention_pb_k_kernel(
     with ExitStack() as stack:
         keep = stack.enter_context(tc.tile_pool(name="keep", bufs=1))
         raw_pool = stack.enter_context(tc.tile_pool(name="raw", bufs=CV_RAW_BUFS))
+        halves_pool = stack.enter_context(tc.tile_pool(name="halves", bufs=2))
         grouped_pool = stack.enter_context(tc.tile_pool(name="grouped", bufs=2))
         codes_pool = stack.enter_context(tc.tile_pool(name="codes", bufs=CV_LEAD + 1))
         soft_pool = stack.enter_context(tc.tile_pool(name="soft", bufs=2))
@@ -78,6 +79,7 @@ def tile_multiheadlatentattention_pb_k_kernel(
         v_scales = keep.tile([P, BATCHES, V_WIDTH], U8, align_bytes=64)
 
         cv_raw_of = {}
+        cv_halves_of = {}
         grouped_of = {}
         cv_codes_of = {}
         v_acc_of = {}
@@ -118,22 +120,27 @@ def tile_multiheadlatentattention_pb_k_kernel(
                 in_=W_v_dec_words[passes].rearrange("g p n t -> p g (n t)").bitcast(I32),
             )
 
+        def split_cv(i):
+            if not 0 <= i < ROUNDS:
+                return
+            halves = halves_pool.tile([P, ROUND_PASSES, 2, P], F32)
+            nc.vector.tensor_copy(
+                out=halves[:], in_=cv_raw_of[i][:].bitcast(F32).rearrange("q (g p u) -> q g u p", u=2, p=P)
+            )
+            cv_halves_of[i] = halves
+
         def transpose_cv(i):
             if not 0 <= i < ROUNDS:
                 return
-            cv_words = cv_raw_of[i][:].bitcast(F32)
+            halves = cv_halves_of[i]
             grouped = grouped_pool.tile([P, ROUND_PASSES, P, PACK], BF16, align_bytes=64)
             banks = ROUND_PASSES // 2
             for c in range(banks):
                 bank = work_psum.tile([P, 2, 2, P], F32, tag="work")
                 for g in range(2):
-                    first = (2 * c + g) * WORDS_PER_PASS
                     for u in range(2):
-                        nc.tensor.transpose(
-                            bank[:, g, u, :], cv_words[:, first + u : first + WORDS_PER_PASS : 2], ident_f32[:]
-                        )
-                copy = nc.vector.tensor_copy if c == banks - 1 else nc.scalar.copy
-                copy(out=grouped[:, 2 * c : 2 * c + 2].bitcast(F32), in_=bank[:].rearrange("p g u t -> p g t u"))
+                        nc.tensor.transpose(bank[:, g, u, :], halves[:, 2 * c + g, u, :], ident_f32[:])
+                nc.scalar.copy(out=grouped[:, 2 * c : 2 * c + 2].bitcast(F32), in_=bank[:].rearrange("p g u t -> p g t u"))
             grouped_of[i] = grouped
 
         def quantise_cv(i):
@@ -306,12 +313,13 @@ def tile_multiheadlatentattention_pb_k_kernel(
             load_cv(i)
         load_qk(1)
 
-        first_turn = -max(ATTENTION_LEAD + 2, CV_LEAD)
+        first_turn = -max(ATTENTION_LEAD + 2, CV_LEAD + 1)
         for turn in range(first_turn, ROUNDS + ROW_TILES):
             step = turn + ATTENTION_LEAD
-            freed = turn + CV_LEAD - 1
+            freed = turn + CV_LEAD
             if freed >= 0:
                 load_cv(freed + CV_RAW_BUFS)
+            split_cv(turn + CV_LEAD + 1)
             transpose_cv(turn + CV_LEAD)
             scores(step + 1)
             if step % STEPS_PER_HEAD == 0:

@@ -250,7 +250,7 @@ def tile_multiheadlatentattention_pb_k_kernel(
                 for u in range(2):
                     nc.tensor.transpose(e_bank[:, a, u, :], e_words[:, u * P : (u + 1) * P], ident_f32[:])
             e_grouped = soft_pool.tile([P, STEP_TILES, P, PACK], BF16, align_bytes=64)
-            nc.vector.tensor_copy(out=e_grouped[:].bitcast(F32), in_=e_bank[:].rearrange("p a u q -> p a q u"))
+            nc.scalar.copy(out=e_grouped[:].bitcast(F32), in_=e_bank[:].rearrange("p a u q -> p a q u"))
             e_grouped_of[step] = e_grouped
 
         def quantise_e(step):

@@ -24,7 +24,8 @@ V_WIDTH = HEADS * HEAD_DIM
 
 PASSES = LATENT // K_PASS
 ROW_TILES = TOKENS // P
-ROUND_PASSES = 8
+ROUND_PASSES = 4
+ROUND_BANKS = ROUND_PASSES // 2
 ROUNDS_PER_TILE = PASSES // ROUND_PASSES
 ROUNDS_PER_BATCH = ROW_TILES * ROUNDS_PER_TILE
 ROUNDS = BATCHES * ROUNDS_PER_BATCH
@@ -35,9 +36,14 @@ STEP_TILES = 2
 STEPS_PER_HEAD = ROW_TILES // STEP_TILES
 STEPS = BATCHES * HEADS * STEPS_PER_HEAD
 
-CV_LEAD = 3
-ATTENTION_LEAD = 3
-CV_RAW_BUFS = 5
+CV_LEAD = 2
+ATTENTION_LEAD = 1
+LOAD_ROUNDS = 2
+LOADS = ROUNDS // LOAD_ROUNDS
+CV_RAW_BUFS = 6
+SPLIT = "1"
+VBANK = "0"
+EC = "s"
 
 SOFTMAX_SCALE = 1.0 / math.sqrt(HEAD_DIM)
 
@@ -51,10 +57,10 @@ def tile_multiheadlatentattention_pb_k_kernel(
     with ExitStack() as stack:
         keep = stack.enter_context(tc.tile_pool(name="keep", bufs=1))
         raw_pool = stack.enter_context(tc.tile_pool(name="raw", bufs=CV_RAW_BUFS))
-        halves_pool = stack.enter_context(tc.tile_pool(name="halves", bufs=2))
-        grouped_pool = stack.enter_context(tc.tile_pool(name="grouped", bufs=2))
-        codes_pool = stack.enter_context(tc.tile_pool(name="codes", bufs=CV_LEAD + 1))
-        soft_pool = stack.enter_context(tc.tile_pool(name="soft", bufs=2))
+        halves_pool = stack.enter_context(tc.tile_pool(name="halves", bufs=3))
+        grouped_pool = stack.enter_context(tc.tile_pool(name="grouped", bufs=3))
+        codes_pool = stack.enter_context(tc.tile_pool(name="codes", bufs=CV_LEAD + 2))
+        soft_pool = stack.enter_context(tc.tile_pool(name="soft", bufs=3))
         small_pool = stack.enter_context(tc.tile_pool(name="small", bufs=3))
         out_pool = stack.enter_context(tc.tile_pool(name="result", bufs=ROW_TILES))
         work_psum = stack.enter_context(tc.psum_pool(name="work", bufs=4))
@@ -83,6 +89,7 @@ def tile_multiheadlatentattention_pb_k_kernel(
         grouped_of = {}
         cv_codes_of = {}
         v_acc_of = {}
+        peak_of = {}
         score_of = {}
         shift_of = {}
         e_rows_of = {}
@@ -94,23 +101,28 @@ def tile_multiheadlatentattention_pb_k_kernel(
             nc.sync.dma_start(out=q_rows[:, b], in_=q_rot[b].rearrange("(i p) h d -> p i (h d)", p=P))
             nc.sync.dma_start(out=k_rows[:, b], in_=k_rot[b].rearrange("(i p) h d -> p i (h d)", p=P))
 
-        def load_cv(i):
-            if not 0 <= i < ROUNDS:
+        def load_cv(n, parts=1):
+            if not 0 <= n < LOADS:
                 return
-            row_tile, half = divmod(i, ROUNDS_PER_TILE)
+            row_tile, part = divmod(n, LOADS // (BATCHES * ROW_TILES))
             b, j = divmod(row_tile, ROW_TILES)
             u, e = divmod(j, 2)
-            cv_raw = raw_pool.tile([P, ROUND_K], BF16)
-            nc.sync.dma_start(out=cv_raw[:], in_=cv_tiles[b, u, e, :, half * ROUND_K : (half + 1) * ROUND_K])
-            cv_raw_of[i] = cv_raw
+            cv_raw = raw_pool.tile([P, LOAD_ROUNDS * ROUND_K], BF16)
+            width = LOAD_ROUNDS * ROUND_K // parts
+            for h in range(parts):
+                first = part * LOAD_ROUNDS * ROUND_K + h * width
+                nc.sync.dma_start(
+                    out=cv_raw[:, h * width : (h + 1) * width], in_=cv_tiles[b, u, e, :, first : first + width]
+                )
+            cv_raw_of[n] = cv_raw
 
         def load_w_scales():
             for quadrant in range(4):
-                nc.gpsimd.dma_start(
-                    out=w_scales[32 * quadrant : 32 * quadrant + 4].bitcast(F32),
+                nc.sync.dma_start(
+                    out=w_scales[32 * quadrant : 32 * quadrant + 4].bitcast(I32),
                     in_=W_v_dec_scales[:, 4 * quadrant : 4 * quadrant + 4, :]
                     .rearrange("g r n -> r g n")
-                    .bitcast(F32),
+                    .bitcast(I32),
                 )
 
         def load_w_words(first_pass, n_passes):
@@ -120,27 +132,37 @@ def tile_multiheadlatentattention_pb_k_kernel(
                 in_=W_v_dec_words[passes].rearrange("g p n t -> p g (n t)").bitcast(I32),
             )
 
+        def raw_words(i):
+            n, h = divmod(i, LOAD_ROUNDS)
+            return cv_raw_of[n][:, h * ROUND_K : (h + 1) * ROUND_K].bitcast(F32)
+
+        def is_split(i):
+            return SPLIT[i % len(SPLIT)] == "1"
+
         def split_cv(i):
-            if not 0 <= i < ROUNDS:
+            if not 0 <= i < ROUNDS or not is_split(i):
                 return
             halves = halves_pool.tile([P, ROUND_PASSES, 2, P], F32)
-            nc.vector.tensor_copy(
-                out=halves[:], in_=cv_raw_of[i][:].bitcast(F32).rearrange("q (g p u) -> q g u p", u=2, p=P)
-            )
+            nc.vector.tensor_copy(out=halves[:], in_=raw_words(i).rearrange("q (g p u) -> q g u p", u=2, p=P))
             cv_halves_of[i] = halves
 
         def transpose_cv(i):
             if not 0 <= i < ROUNDS:
                 return
-            halves = cv_halves_of[i]
             grouped = grouped_pool.tile([P, ROUND_PASSES, P, PACK], BF16, align_bytes=64)
-            banks = ROUND_PASSES // 2
-            for c in range(banks):
+            for c in range(ROUND_BANKS):
                 bank = work_psum.tile([P, 2, 2, P], F32, tag="work")
                 for g in range(2):
+                    first = (2 * c + g) * WORDS_PER_PASS
                     for u in range(2):
-                        nc.tensor.transpose(bank[:, g, u, :], halves[:, 2 * c + g, u, :], ident_f32[:])
-                nc.scalar.copy(out=grouped[:, 2 * c : 2 * c + 2].bitcast(F32), in_=bank[:].rearrange("p g u t -> p g t u"))
+                        if is_split(i):
+                            words = cv_halves_of[i][:, 2 * c + g, u, :]
+                        else:
+                            words = raw_words(i)[:, first + u : first + WORDS_PER_PASS : 2]
+                        nc.tensor.transpose(bank[:, g, u, :], words, ident_f32[:])
+                index = i * ROUND_BANKS + c
+                copy = nc.vector.tensor_copy if VBANK[index % len(VBANK)] == "1" else nc.scalar.copy
+                copy(out=grouped[:, 2 * c : 2 * c + 2].bitcast(F32), in_=bank[:].rearrange("p g u t -> p g t u"))
             grouped_of[i] = grouped
 
         def quantise_cv(i):
@@ -158,14 +180,14 @@ def tile_multiheadlatentattention_pb_k_kernel(
         def project(i):
             if not 0 <= i < ROUNDS:
                 return
-            row_tile, half = divmod(i, ROUNDS_PER_TILE)
-            if half == 0:
+            row_tile, part = divmod(i, ROUNDS_PER_TILE)
+            if part == 0:
                 v_acc = v_psum.tile([P, V_WIDTH], F32)
                 v_acc_of[row_tile] = v_acc
             v_acc = v_acc_of[row_tile]
             cv_codes, cv_scales = cv_codes_of[i]
             for g in range(ROUND_PASSES):
-                k_pass = half * ROUND_PASSES + g
+                k_pass = part * ROUND_PASSES + g
                 tokens = slice(g * P, (g + 1) * P)
                 nc.tensor.matmul_mx(
                     out=v_acc[:],
@@ -176,10 +198,13 @@ def tile_multiheadlatentattention_pb_k_kernel(
                     start=(k_pass == 0),
                     stop=(k_pass == PASSES - 1),
                 )
-            if half < ROUNDS_PER_TILE - 1:
+
+        def hand_on_v(i):
+            row_tile, part = divmod(i, ROUNDS_PER_TILE)
+            if not 0 <= i < ROUNDS or part < ROUNDS_PER_TILE - 1:
                 return
             b, j = divmod(row_tile, ROW_TILES)
-            nc.scalar.copy(out=v_rows[:, b, j, :], in_=v_acc[:])
+            nc.scalar.copy(out=v_rows[:, b, j, :], in_=v_acc_of[row_tile][:])
             if j == ROW_TILES - 1:
                 nc.vector.tensor_copy(out=v_grouped[:, b], in_=v_rows[:, b].rearrange("p j n -> p n j"))
                 nc.vector.quantize_mx(
@@ -219,8 +244,13 @@ def tile_multiheadlatentattention_pb_k_kernel(
                     out=peak[:, a : a + 1], in_=score[:], axis=mybir.AxisListType.X, op=mybir.AluOpType.max
                 )
                 score_of[(step, a)] = score
+            peak_of[step] = peak
+
+        def shifts(step):
+            if not 0 <= step < STEPS:
+                return
             shift = small_pool.tile([P, STEP_TILES], F32)
-            nc.vector.tensor_scalar_mul(out=shift[:], in0=peak[:], scalar1=-SOFTMAX_SCALE)
+            nc.vector.tensor_scalar_mul(out=shift[:], in0=peak_of[step][:], scalar1=-SOFTMAX_SCALE)
             shift_of[step] = shift
 
         def exponentials(step):
@@ -250,7 +280,8 @@ def tile_multiheadlatentattention_pb_k_kernel(
                 for u in range(2):
                     nc.tensor.transpose(e_bank[:, a, u, :], e_words[:, u * P : (u + 1) * P], ident_f32[:])
             e_grouped = soft_pool.tile([P, STEP_TILES, P, PACK], BF16, align_bytes=64)
-            nc.scalar.copy(out=e_grouped[:].bitcast(F32), in_=e_bank[:].rearrange("p a u q -> p a q u"))
+            copy = nc.vector.tensor_copy if EC[step % len(EC)] == "v" else nc.scalar.copy
+            copy(out=e_grouped[:].bitcast(F32), in_=e_bank[:].rearrange("p a u q -> p a q u"))
             e_grouped_of[step] = e_grouped
 
         def quantise_e(step):
@@ -267,20 +298,18 @@ def tile_multiheadlatentattention_pb_k_kernel(
                 nc.vector.reciprocal(out=inverse_sums[:, tiles, :], in_=row_sums[:, tiles, :])
 
         def context(b, i):
-            if not (0 <= b < BATCHES and i < ROW_TILES):
-                return
             pair, a = divmod(i, STEP_TILES)
             queries = slice(a * P, (a + 1) * P)
             ctx_bank = work_psum.tile([P, HEADS, HEAD_DIM], F32, tag="work")
             for h in range(HEADS):
                 step = (b * HEADS + h) * STEPS_PER_HEAD + pair
-                head = slice(h * HEAD_DIM, (h + 1) * HEAD_DIM)
+                cols = slice(h * HEAD_DIM, (h + 1) * HEAD_DIM)
                 nc.tensor.matmul_mx(
                     out=ctx_bank[:, h, :],
                     lhsT=e_codes[:, step, queries].bitcast(FP8X4),
                     lhsT_scale=e_scales[:, step, queries],
-                    rhs=v_codes[:, b, head].bitcast(FP8X4),
-                    rhs_scale=v_scales[:, b, head],
+                    rhs=v_codes[:, b, cols].bitcast(FP8X4),
+                    rhs_scale=v_scales[:, b, cols],
                     start=True,
                     stop=True,
                 )
@@ -300,34 +329,42 @@ def tile_multiheadlatentattention_pb_k_kernel(
         nc.scalar.activation(out=warm[:], in_=warm[:], func=mybir.ActivationFunctionType.Exp)
         make_identity(nc, ident_bf16[:])
         make_identity(nc, ident_f32[:])
-        load_w_scales()
         load_qk(0)
-        for i in range(CV_LEAD + 1):
-            load_cv(i)
-        load_w_words(0, 4)
-        load_w_words(4, 4)
-        load_cv(CV_LEAD + 1)
-        load_w_words(8, 4)
-        load_w_words(12, 4)
-        for i in range(CV_LEAD + 2, CV_RAW_BUFS):
-            load_cv(i)
-        load_qk(1)
+        loaded = 0
+        for c in "ccs01c23ccq":
+            if c == "q":
+                load_qk(1)
+            elif c == "s":
+                load_w_scales()
+            elif c == "c":
+                load_cv(loaded, 2 if loaded == 0 else 1)
+                loaded += 1
+            else:
+                load_w_words(4 * int(c), 4)
+        for n in range(loaded, CV_RAW_BUFS):
+            load_cv(n)
 
-        first_turn = -max(ATTENTION_LEAD + 2, CV_LEAD + 1)
-        for turn in range(first_turn, ROUNDS + ROW_TILES):
-            step = turn + ATTENTION_LEAD
+        first_turn = -max(2 * ATTENTION_LEAD + 4, CV_LEAD + 1)
+        for turn in range(first_turn, ROUNDS + 2 * ROW_TILES):
+            step, odd = divmod(turn + 2 * ATTENTION_LEAD, 2)
             freed = turn + CV_LEAD
-            if freed >= 0:
-                load_cv(freed + CV_RAW_BUFS)
+            if freed > 0 and freed % LOAD_ROUNDS == 0:
+                load_cv(freed // LOAD_ROUNDS - 1 + CV_RAW_BUFS)
             split_cv(turn + CV_LEAD + 1)
             transpose_cv(turn + CV_LEAD)
-            scores(step + 1)
-            if step % STEPS_PER_HEAD == 0:
-                transpose_qk(step // STEPS_PER_HEAD + 1)
-            transpose_e(step)
-            exponentials(step + 1)
-            quantise_e(step)
+            if odd:
+                quantise_e(step - 1)
+                if step % STEPS_PER_HEAD == 0:
+                    transpose_qk(step // STEPS_PER_HEAD + 1)
+                scores(step + 1)
+            else:
+                transpose_e(step - 1)
+                exponentials(step)
             quantise_cv(turn + CV_LEAD)
+            if odd:
+                shifts(step + 1)
             project(turn)
-            b, i = divmod(turn - ROUNDS_PER_BATCH, ROUNDS_PER_BATCH)
-            context(b, i)
+            hand_on_v(turn)
+            late = turn - ROUNDS_PER_BATCH
+            if late >= 0 and late % ROUNDS_PER_BATCH < 2 * ROW_TILES and late % 2 == 0:
+                context(late // ROUNDS_PER_BATCH, late % ROUNDS_PER_BATCH // 2)

@@ -41,9 +41,13 @@ ATTENTION_LEAD = 1
 LOAD_ROUNDS = 2
 LOADS = ROUNDS // LOAD_ROUNDS
 CV_RAW_BUFS = 6
-SPLIT = "1"
-VBANK = "0"
-EC = "s"
+TAIL = 1
+LAST_TILE = BATCHES * ROW_TILES - 1
+GROUP_HEADS = 2
+GROUPS = HEADS // GROUP_HEADS
+GROUP = GROUP_HEADS * HEAD_DIM
+VBANK = "0001"
+EC = "v"
 
 SOFTMAX_SCALE = 1.0 / math.sqrt(HEAD_DIM)
 
@@ -57,9 +61,8 @@ def tile_multiheadlatentattention_pb_k_kernel(
     with ExitStack() as stack:
         keep = stack.enter_context(tc.tile_pool(name="keep", bufs=1))
         raw_pool = stack.enter_context(tc.tile_pool(name="raw", bufs=CV_RAW_BUFS))
-        halves_pool = stack.enter_context(tc.tile_pool(name="halves", bufs=3))
         grouped_pool = stack.enter_context(tc.tile_pool(name="grouped", bufs=3))
-        codes_pool = stack.enter_context(tc.tile_pool(name="codes", bufs=CV_LEAD + 2))
+        codes_pool = stack.enter_context(tc.tile_pool(name="codes", bufs=CV_LEAD + 4))
         soft_pool = stack.enter_context(tc.tile_pool(name="soft", bufs=3))
         small_pool = stack.enter_context(tc.tile_pool(name="small", bufs=3))
         out_pool = stack.enter_context(tc.tile_pool(name="result", bufs=ROW_TILES))
@@ -85,7 +88,6 @@ def tile_multiheadlatentattention_pb_k_kernel(
         v_scales = keep.tile([P, BATCHES, V_WIDTH], U8, align_bytes=64)
 
         cv_raw_of = {}
-        cv_halves_of = {}
         grouped_of = {}
         cv_codes_of = {}
         v_acc_of = {}
@@ -136,16 +138,6 @@ def tile_multiheadlatentattention_pb_k_kernel(
             n, h = divmod(i, LOAD_ROUNDS)
             return cv_raw_of[n][:, h * ROUND_K : (h + 1) * ROUND_K].bitcast(F32)
 
-        def is_split(i):
-            return SPLIT[i % len(SPLIT)] == "1"
-
-        def split_cv(i):
-            if not 0 <= i < ROUNDS or not is_split(i):
-                return
-            halves = halves_pool.tile([P, ROUND_PASSES, 2, P], F32)
-            nc.vector.tensor_copy(out=halves[:], in_=raw_words(i).rearrange("q (g p u) -> q g u p", u=2, p=P))
-            cv_halves_of[i] = halves
-
         def transpose_cv(i):
             if not 0 <= i < ROUNDS:
                 return
@@ -155,11 +147,9 @@ def tile_multiheadlatentattention_pb_k_kernel(
                 for g in range(2):
                     first = (2 * c + g) * WORDS_PER_PASS
                     for u in range(2):
-                        if is_split(i):
-                            words = cv_halves_of[i][:, 2 * c + g, u, :]
-                        else:
-                            words = raw_words(i)[:, first + u : first + WORDS_PER_PASS : 2]
-                        nc.tensor.transpose(bank[:, g, u, :], words, ident_f32[:])
+                        nc.tensor.transpose(
+                            bank[:, g, u, :], raw_words(i)[:, first + u : first + WORDS_PER_PASS : 2], ident_f32[:]
+                        )
                 index = i * ROUND_BANKS + c
                 copy = nc.vector.tensor_copy if VBANK[index % len(VBANK)] == "1" else nc.scalar.copy
                 copy(out=grouped[:, 2 * c : 2 * c + 2].bitcast(F32), in_=bank[:].rearrange("p g u t -> p g t u"))
@@ -178,9 +168,9 @@ def tile_multiheadlatentattention_pb_k_kernel(
             cv_codes_of[i] = (cv_codes, cv_scales)
 
         def project(i):
-            if not 0 <= i < ROUNDS:
-                return
             row_tile, part = divmod(i, ROUNDS_PER_TILE)
+            if not 0 <= i < ROUNDS or (TAIL and row_tile == LAST_TILE):
+                return
             if part == 0:
                 v_acc = v_psum.tile([P, V_WIDTH], F32)
                 v_acc_of[row_tile] = v_acc
@@ -199,19 +189,106 @@ def tile_multiheadlatentattention_pb_k_kernel(
                     stop=(k_pass == PASSES - 1),
                 )
 
+        def project_half(part, c):
+            if part == 0:
+                v_acc = v_psum.tile([P, GROUP], F32)
+                v_acc_of[(LAST_TILE, c)] = v_acc
+            v_acc = v_acc_of[(LAST_TILE, c)]
+            cols = slice(c * GROUP, (c + 1) * GROUP)
+            cv_codes, cv_scales = cv_codes_of[LAST_TILE * ROUNDS_PER_TILE + part]
+            for g in range(ROUND_PASSES):
+                k_pass = part * ROUND_PASSES + g
+                tokens = slice(g * P, (g + 1) * P)
+                nc.tensor.matmul_mx(
+                    out=v_acc[:],
+                    lhsT=cv_codes[:, tokens].bitcast(FP8X4),
+                    lhsT_scale=cv_scales[:, tokens],
+                    rhs=w_words[:, k_pass, PACK * c * GROUP : PACK * (c + 1) * GROUP].bitcast(FP8X4),
+                    rhs_scale=w_scales[:, k_pass, cols],
+                    start=(k_pass == 0),
+                    stop=(k_pass == PASSES - 1),
+                )
+
+        def regroup_v(b, first, width):
+            cols = slice(first, first + width)
+            nc.vector.tensor_copy(out=v_grouped[:, b, cols, :], in_=v_rows[:, b, :, cols].rearrange("p j n -> p n j"))
+
+        def quantise_v(b, first, width):
+            cols = slice(first, first + width)
+            nc.vector.quantize_mx(
+                out=v_codes[:, b, cols].bitcast(FP8X4),
+                scales=v_scales[:, b, cols],
+                in_=v_grouped[:, b, cols, :].rearrange("p n j -> p (n j)"),
+            )
+
         def hand_on_v(i):
             row_tile, part = divmod(i, ROUNDS_PER_TILE)
-            if not 0 <= i < ROUNDS or part < ROUNDS_PER_TILE - 1:
+            if not 0 <= i < ROUNDS or part < ROUNDS_PER_TILE - 1 or (TAIL and row_tile == LAST_TILE):
                 return
             b, j = divmod(row_tile, ROW_TILES)
             nc.scalar.copy(out=v_rows[:, b, j, :], in_=v_acc_of[row_tile][:])
-            if j == ROW_TILES - 1:
-                nc.vector.tensor_copy(out=v_grouped[:, b], in_=v_rows[:, b].rearrange("p j n -> p n j"))
-                nc.vector.quantize_mx(
-                    out=v_codes[:, b, :].bitcast(FP8X4),
-                    scales=v_scales[:, b, :],
-                    in_=v_grouped[:, b].rearrange("p n j -> p (n j)"),
+            if j == ROW_TILES - 1 and not (TAIL and b == 0):
+                regroup_v(b, 0, V_WIDTH)
+                quantise_v(b, 0, V_WIDTH)
+
+        def spread_v(turn):
+            h = turn - ROUNDS_PER_BATCH
+            if not TAIL:
+                return
+            if 0 <= h - 1 < HEADS:
+                quantise_v(0, (h - 1) * HEAD_DIM, HEAD_DIM)
+            if 0 <= h < HEADS:
+                regroup_v(0, h * HEAD_DIM, HEAD_DIM)
+
+        def hand_on_half(c):
+            first = c * GROUP
+            nc.scalar.copy(out=v_rows[:, BATCHES - 1, ROW_TILES - 1, first : first + GROUP], in_=v_acc_of[(LAST_TILE, c)][:])
+            regroup_v(BATCHES - 1, first, GROUP)
+            quantise_v(BATCHES - 1, first, GROUP)
+
+        def context_half(c, pair):
+            b = BATCHES - 1
+            heads = slice(c * GROUP_HEADS, (c + 1) * GROUP_HEADS)
+            ctx_bank = work_psum.tile([P, STEP_TILES, GROUP_HEADS, HEAD_DIM], F32, tag="work")
+            for h2 in range(GROUP_HEADS):
+                h = c * GROUP_HEADS + h2
+                step = (b * HEADS + h) * STEPS_PER_HEAD + pair
+                cols = slice(h * HEAD_DIM, (h + 1) * HEAD_DIM)
+                for a in range(STEP_TILES):
+                    queries = slice(a * P, (a + 1) * P)
+                    nc.tensor.matmul_mx(
+                        out=ctx_bank[:, a, h2, :],
+                        lhsT=e_codes[:, step, queries].bitcast(FP8X4),
+                        lhsT_scale=e_scales[:, step, queries],
+                        rhs=v_codes[:, b, cols].bitcast(FP8X4),
+                        rhs_scale=v_scales[:, b, cols],
+                        start=True,
+                        stop=True,
+                    )
+            first = b * ROW_TILES + pair * STEP_TILES
+            ctx_rows = out_pool.tile([P, STEP_TILES, GROUP_HEADS, HEAD_DIM], F32)
+            if c == 1 and pair == 1 and TAIL == 2:
+                for a in range(STEP_TILES):
+                    for h2 in range(GROUP_HEADS):
+                        h = c * GROUP_HEADS + h2
+                        nc.scalar.activation(
+                            out=ctx_rows[:, a, h2, :],
+                            in_=ctx_bank[:, a, h2, :],
+                            func=mybir.ActivationFunctionType.Copy,
+                            scale=inverse_sums[:, first + a, h : h + 1],
+                        )
+            else:
+                inverse = inverse_sums[:, first : first + STEP_TILES, heads]
+                nc.vector.tensor_tensor(
+                    out=ctx_rows[:],
+                    in0=ctx_bank[:],
+                    in1=inverse.unsqueeze(3).to_broadcast([P, STEP_TILES, GROUP_HEADS, HEAD_DIM]),
+                    op=mybir.AluOpType.mult,
                 )
+            rows = out[b, pair * STEP_TILES * P : (pair + 1) * STEP_TILES * P, c * GROUP : (c + 1) * GROUP]
+            nc.sync.dma_start(
+                out=rows.rearrange("(a p) d -> p a d", p=P), in_=ctx_rows[:].rearrange("p a h d -> p a (h d)")
+            )
 
         def transpose_qk(head_block):
             if not 0 <= head_block < BATCHES * HEADS:
@@ -323,12 +400,12 @@ def tile_multiheadlatentattention_pb_k_kernel(
             )
             nc.sync.dma_start(out=out[b, i * P : (i + 1) * P, :], in_=ctx_rows[:].rearrange("p h d -> p (h d)"))
 
-        nc.vector.memset(w_scales[:].rearrange("p g n -> p (g n)").bitcast(I32), 0)
         warm = small_pool.tile([P, 1], F32)
         nc.vector.memset(warm[:], 0.0)
         nc.scalar.activation(out=warm[:], in_=warm[:], func=mybir.ActivationFunctionType.Exp)
         make_identity(nc, ident_bf16[:])
         make_identity(nc, ident_f32[:])
+        nc.vector.memset(w_scales[:].rearrange("p g n -> p (g n)").bitcast(I32), 0)
         load_qk(0)
         loaded = 0
         for c in "ccs01c23ccq":
@@ -344,13 +421,13 @@ def tile_multiheadlatentattention_pb_k_kernel(
         for n in range(loaded, CV_RAW_BUFS):
             load_cv(n)
 
+        halves_at = {0: ((0, 0), (1, 0)), 1: ((2, 0), (0, 1)), 2: ((3, 0), (1, 1)), 3: ((2, 1), (3, 1))}
         first_turn = -max(2 * ATTENTION_LEAD + 4, CV_LEAD + 1)
         for turn in range(first_turn, ROUNDS + 2 * ROW_TILES):
             step, odd = divmod(turn + 2 * ATTENTION_LEAD, 2)
             freed = turn + CV_LEAD
             if freed > 0 and freed % LOAD_ROUNDS == 0:
                 load_cv(freed // LOAD_ROUNDS - 1 + CV_RAW_BUFS)
-            split_cv(turn + CV_LEAD + 1)
             transpose_cv(turn + CV_LEAD)
             if odd:
                 quantise_e(step - 1)
@@ -365,6 +442,16 @@ def tile_multiheadlatentattention_pb_k_kernel(
                 shifts(step + 1)
             project(turn)
             hand_on_v(turn)
-            late = turn - ROUNDS_PER_BATCH
-            if late >= 0 and late % ROUNDS_PER_BATCH < 2 * ROW_TILES and late % 2 == 0:
+            spread_v(turn)
+            last = turn - LAST_TILE * ROUNDS_PER_TILE
+            if TAIL and last in halves_at:
+                for part, c in halves_at[last]:
+                    project_half(part, c)
+                    if part == ROUNDS_PER_TILE - 1:
+                        hand_on_half(c)
+            if TAIL and last in (4, 5):
+                for pair in range(STEPS_PER_HEAD):
+                    context_half(last - 4, pair)
+            late = turn - ROUNDS_PER_BATCH - 4
+            if late >= 0 and (not TAIL or turn < ROUNDS) and late % ROUNDS_PER_BATCH < 2 * ROW_TILES and late % 2 == 0:
                 context(late // ROUNDS_PER_BATCH, late % ROUNDS_PER_BATCH // 2)

@@ -24,7 +24,7 @@ V_WIDTH = HEADS * HEAD_DIM
 
 PASSES = LATENT // K_PASS
 ROW_TILES = TOKENS // P
-ROUND_PASSES = 4
+ROUND_PASSES = 8
 ROUND_BANKS = ROUND_PASSES // 2
 ROUNDS_PER_TILE = PASSES // ROUND_PASSES
 ROUNDS_PER_BATCH = ROW_TILES * ROUNDS_PER_TILE
@@ -38,7 +38,7 @@ STEPS = BATCHES * HEADS * STEPS_PER_HEAD
 
 CV_LEAD = 2
 ATTENTION_LEAD = 1
-LOAD_ROUNDS = 2
+LOAD_ROUNDS = 1
 LOADS = ROUNDS // LOAD_ROUNDS
 CV_RAW_BUFS = 6
 TAIL = 1
@@ -46,7 +46,7 @@ LAST_TILE = BATCHES * ROW_TILES - 1
 GROUP_HEADS = 2
 GROUPS = HEADS // GROUP_HEADS
 GROUP = GROUP_HEADS * HEAD_DIM
-VBANK = "0001"
+VBANK = "0"
 EC = "v"
 
 SOFTMAX_SCALE = 1.0 / math.sqrt(HEAD_DIM)
@@ -61,8 +61,8 @@ def tile_multiheadlatentattention_pb_k_kernel(
     with ExitStack() as stack:
         keep = stack.enter_context(tc.tile_pool(name="keep", bufs=1))
         raw_pool = stack.enter_context(tc.tile_pool(name="raw", bufs=CV_RAW_BUFS))
-        grouped_pool = stack.enter_context(tc.tile_pool(name="grouped", bufs=3))
-        codes_pool = stack.enter_context(tc.tile_pool(name="codes", bufs=CV_LEAD + 4))
+        grouped_pool = stack.enter_context(tc.tile_pool(name="grouped", bufs=2))
+        codes_pool = stack.enter_context(tc.tile_pool(name="codes", bufs=CV_LEAD + 2))
         soft_pool = stack.enter_context(tc.tile_pool(name="soft", bufs=3))
         small_pool = stack.enter_context(tc.tile_pool(name="small", bufs=3))
         out_pool = stack.enter_context(tc.tile_pool(name="result", bufs=ROW_TILES))
@@ -138,11 +138,14 @@ def tile_multiheadlatentattention_pb_k_kernel(
             n, h = divmod(i, LOAD_ROUNDS)
             return cv_raw_of[n][:, h * ROUND_K : (h + 1) * ROUND_K].bitcast(F32)
 
-        def transpose_cv(i):
+        def transpose_cv(i, first_bank, last_bank):
             if not 0 <= i < ROUNDS:
                 return
-            grouped = grouped_pool.tile([P, ROUND_PASSES, P, PACK], BF16, align_bytes=64)
-            for c in range(ROUND_BANKS):
+            if first_bank == 0:
+                grouped = grouped_pool.tile([P, ROUND_PASSES, P, PACK], BF16, align_bytes=64)
+                grouped_of[i] = grouped
+            grouped = grouped_of[i]
+            for c in range(first_bank, last_bank):
                 bank = work_psum.tile([P, 2, 2, P], F32, tag="work")
                 for g in range(2):
                     first = (2 * c + g) * WORDS_PER_PASS
@@ -150,22 +153,24 @@ def tile_multiheadlatentattention_pb_k_kernel(
                         nc.tensor.transpose(
                             bank[:, g, u, :], raw_words(i)[:, first + u : first + WORDS_PER_PASS : 2], ident_f32[:]
                         )
-                index = i * ROUND_BANKS + c
-                copy = nc.vector.tensor_copy if VBANK[index % len(VBANK)] == "1" else nc.scalar.copy
+                copy = nc.vector.tensor_copy if VBANK[c % len(VBANK)] == "1" else nc.scalar.copy
                 copy(out=grouped[:, 2 * c : 2 * c + 2].bitcast(F32), in_=bank[:].rearrange("p g u t -> p g t u"))
-            grouped_of[i] = grouped
 
-        def quantise_cv(i):
+        def quantise_cv(i, half=None):
             if not 0 <= i < ROUNDS:
                 return
-            cv_codes = codes_pool.tile([P, ROUND_PASSES * P], U32, align_bytes=64)
-            cv_scales = codes_pool.tile([P, ROUND_PASSES * P], U8, align_bytes=64)
+            if half in (None, 0):
+                cv_codes = codes_pool.tile([P, ROUND_PASSES * P], U32, align_bytes=64)
+                cv_scales = codes_pool.tile([P, ROUND_PASSES * P], U8, align_bytes=64)
+                cv_codes_of[i] = (cv_codes, cv_scales)
+            cv_codes, cv_scales = cv_codes_of[i]
+            passes = slice(0, ROUND_PASSES) if half is None else slice(half * ROUND_PASSES // 2, (half + 1) * ROUND_PASSES // 2)
+            cols = slice(passes.start * P, passes.stop * P)
             nc.vector.quantize_mx(
-                out=cv_codes[:].bitcast(FP8X4),
-                scales=cv_scales[:],
-                in_=grouped_of[i][:].rearrange("p g t j -> p (g t j)"),
+                out=cv_codes[:, cols].bitcast(FP8X4),
+                scales=cv_scales[:, cols],
+                in_=grouped_of[i][:, passes].rearrange("p g t j -> p (g t j)"),
             )
-            cv_codes_of[i] = (cv_codes, cv_scales)
 
         def project(i):
             row_tile, part = divmod(i, ROUNDS_PER_TILE)
@@ -302,51 +307,54 @@ def tile_multiheadlatentattention_pb_k_kernel(
                     )
             nc.scalar.copy(out=qk_t[:, head_block], in_=qk_bank[:])
 
-        def scores(step):
+        def scores(step, a):
             if not 0 <= step < STEPS:
                 return
             head_block, pair = divmod(step, STEPS_PER_HEAD)
-            peak = small_pool.tile([P, STEP_TILES], F32)
-            for a in range(STEP_TILES):
-                i = pair * STEP_TILES + a
-                score = score_psum.tile([P, TOKENS], F32)
-                nc.tensor.matmul(
-                    out=score[:],
-                    lhsT=qk_t[:, head_block, 0, i * P : (i + 1) * P],
-                    rhs=qk_t[:, head_block, 1, :],
-                    start=True,
-                    stop=True,
-                )
-                nc.vector.tensor_reduce(
-                    out=peak[:, a : a + 1], in_=score[:], axis=mybir.AxisListType.X, op=mybir.AluOpType.max
-                )
-                score_of[(step, a)] = score
-            peak_of[step] = peak
+            i = pair * STEP_TILES + a
+            score = score_psum.tile([P, TOKENS], F32)
+            nc.tensor.matmul(
+                out=score[:],
+                lhsT=qk_t[:, head_block, 0, i * P : (i + 1) * P],
+                rhs=qk_t[:, head_block, 1, :],
+                start=True,
+                stop=True,
+            )
+            score_of[(step, a)] = score
 
-        def shifts(step):
+        def maxima(step, a):
             if not 0 <= step < STEPS:
                 return
-            shift = small_pool.tile([P, STEP_TILES], F32)
-            nc.vector.tensor_scalar_mul(out=shift[:], in0=peak_of[step][:], scalar1=-SOFTMAX_SCALE)
-            shift_of[step] = shift
+            peak = small_pool.tile([P, 1], F32)
+            nc.vector.tensor_reduce(
+                out=peak[:], in_=score_of[(step, a)][:], axis=mybir.AxisListType.X, op=mybir.AluOpType.max
+            )
+            peak_of[(step, a)] = peak
 
-        def exponentials(step):
+        def shifts(step, a):
+            if not 0 <= step < STEPS:
+                return
+            shift = small_pool.tile([P, 1], F32)
+            nc.vector.tensor_scalar_mul(out=shift[:], in0=peak_of[(step, a)][:], scalar1=-SOFTMAX_SCALE)
+            shift_of[(step, a)] = shift
+
+        def exponentials(step, a):
             if not 0 <= step < STEPS:
                 return
             head_block, pair = divmod(step, STEPS_PER_HEAD)
             b, h = divmod(head_block, HEADS)
-            e_rows = soft_pool.tile([P, STEP_TILES, TOKENS], BF16)
-            for a in range(STEP_TILES):
-                i = pair * STEP_TILES + a
-                nc.scalar.activation(
-                    out=e_rows[:, a, :],
-                    in_=score_of[(step, a)][:],
-                    func=mybir.ActivationFunctionType.Exp,
-                    bias=shift_of[step][:, a : a + 1],
-                    scale=SOFTMAX_SCALE,
-                    accum_out=row_sums[:, b * ROW_TILES + i, h : h + 1],
-                )
-            e_rows_of[step] = e_rows
+            if a == 0:
+                e_rows = soft_pool.tile([P, STEP_TILES, TOKENS], BF16)
+                e_rows_of[step] = e_rows
+            i = pair * STEP_TILES + a
+            nc.scalar.activation(
+                out=e_rows_of[step][:, a, :],
+                in_=score_of[(step, a)][:],
+                func=mybir.ActivationFunctionType.Exp,
+                bias=shift_of[(step, a)][:],
+                scale=SOFTMAX_SCALE,
+                accum_out=row_sums[:, b * ROW_TILES + i, h : h + 1],
+            )
 
         def transpose_e(step):
             if not 0 <= step < STEPS:
@@ -408,7 +416,7 @@ def tile_multiheadlatentattention_pb_k_kernel(
         nc.vector.memset(w_scales[:].rearrange("p g n -> p (g n)").bitcast(I32), 0)
         load_qk(0)
         loaded = 0
-        for c in "ccs01c23ccq":
+        for c in "ccc0s1c23cq":
             if c == "q":
                 load_qk(1)
             elif c == "s":
@@ -421,25 +429,30 @@ def tile_multiheadlatentattention_pb_k_kernel(
         for n in range(loaded, CV_RAW_BUFS):
             load_cv(n)
 
-        halves_at = {0: ((0, 0), (1, 0)), 1: ((2, 0), (0, 1)), 2: ((3, 0), (1, 1)), 3: ((2, 1), (3, 1))}
-        first_turn = -max(2 * ATTENTION_LEAD + 4, CV_LEAD + 1)
-        for turn in range(first_turn, ROUNDS + 2 * ROW_TILES):
-            step, odd = divmod(turn + 2 * ATTENTION_LEAD, 2)
+        halves_at = {0: ((0, 0),), 1: ((1, 0), (0, 1), (1, 1))}
+        first_turn = -max(ATTENTION_LEAD + 3, CV_LEAD + 1)
+        for turn in range(first_turn, ROUNDS + ROW_TILES):
+            step = turn + ATTENTION_LEAD
+            cv = turn + CV_LEAD
             freed = turn + CV_LEAD
             if freed > 0 and freed % LOAD_ROUNDS == 0:
                 load_cv(freed // LOAD_ROUNDS - 1 + CV_RAW_BUFS)
-            transpose_cv(turn + CV_LEAD)
-            if odd:
-                quantise_e(step - 1)
-                if step % STEPS_PER_HEAD == 0:
-                    transpose_qk(step // STEPS_PER_HEAD + 1)
-                scores(step + 1)
-            else:
-                transpose_e(step - 1)
-                exponentials(step)
-            quantise_cv(turn + CV_LEAD)
-            if odd:
-                shifts(step + 1)
+            transpose_e(step - 1)
+            transpose_cv(cv, 0, 2)
+            scores(step + 1, 0)
+            quantise_e(step - 1)
+            maxima(step + 1, 0)
+            transpose_cv(cv, 2, 4)
+            if step % STEPS_PER_HEAD == 0:
+                transpose_qk(step // STEPS_PER_HEAD + 1)
+            scores(step + 1, 1)
+            quantise_cv(cv, 0)
+            shifts(step + 1, 0)
+            exponentials(step + 1, 0)
+            maxima(step + 1, 1)
+            quantise_cv(cv, 1)
+            shifts(step + 1, 1)
+            exponentials(step + 1, 1)
             project(turn)
             hand_on_v(turn)
             spread_v(turn)
@@ -449,9 +462,9 @@ def tile_multiheadlatentattention_pb_k_kernel(
                     project_half(part, c)
                     if part == ROUNDS_PER_TILE - 1:
                         hand_on_half(c)
-            if TAIL and last in (4, 5):
+            if TAIL and last in (2, 3):
                 for pair in range(STEPS_PER_HEAD):
-                    context_half(last - 4, pair)
+                    context_half(last - 2, pair)
             late = turn - ROUNDS_PER_BATCH - 4
-            if late >= 0 and (not TAIL or turn < ROUNDS) and late % ROUNDS_PER_BATCH < 2 * ROW_TILES and late % 2 == 0:
-                context(late // ROUNDS_PER_BATCH, late % ROUNDS_PER_BATCH // 2)
+            if late >= 0 and (not TAIL or turn < ROUNDS) and late % ROUNDS_PER_BATCH < ROW_TILES:
+                context(late // ROUNDS_PER_BATCH, late % ROUNDS_PER_BATCH)

@@ -41,7 +41,7 @@ ATTENTION_LEAD = 1
 LOAD_ROUNDS = 1
 LOADS = ROUNDS // LOAD_ROUNDS
 CV_RAW_BUFS = 6
-TAIL = 1
+TAIL = 3
 LAST_TILE = BATCHES * ROW_TILES - 1
 GROUP_HEADS = 2
 GROUPS = HEADS // GROUP_HEADS
@@ -65,7 +65,7 @@ def tile_multiheadlatentattention_pb_k_kernel(
         codes_pool = stack.enter_context(tc.tile_pool(name="codes", bufs=CV_LEAD + 2))
         soft_pool = stack.enter_context(tc.tile_pool(name="soft", bufs=3))
         small_pool = stack.enter_context(tc.tile_pool(name="small", bufs=3))
-        out_pool = stack.enter_context(tc.tile_pool(name="result", bufs=ROW_TILES))
+        out_pool = stack.enter_context(tc.tile_pool(name="result", bufs=6))
         work_psum = stack.enter_context(tc.psum_pool(name="work", bufs=4))
         score_psum = stack.enter_context(tc.psum_pool(name="score", bufs=STEP_TILES))
         v_psum = stack.enter_context(tc.psum_pool(name="v", bufs=2))
@@ -237,17 +237,20 @@ def tile_multiheadlatentattention_pb_k_kernel(
                 quantise_v(b, 0, V_WIDTH)
 
         def spread_v(turn):
-            h = turn - ROUNDS_PER_BATCH
+            n = turn - ROUNDS_PER_BATCH
             if not TAIL:
                 return
-            if 0 <= h - 1 < HEADS:
-                quantise_v(0, (h - 1) * HEAD_DIM, HEAD_DIM)
-            if 0 <= h < HEADS:
-                regroup_v(0, h * HEAD_DIM, HEAD_DIM)
+            if 0 <= n - 1 < GROUPS:
+                for h in range((n - 1) * GROUP_HEADS, n * GROUP_HEADS):
+                    quantise_v(0, h * HEAD_DIM, HEAD_DIM)
+            if 0 <= n < GROUPS:
+                for h in range(n * GROUP_HEADS, (n + 1) * GROUP_HEADS):
+                    regroup_v(0, h * HEAD_DIM, HEAD_DIM)
 
         def hand_on_half(c):
             first = c * GROUP
-            nc.scalar.copy(out=v_rows[:, BATCHES - 1, ROW_TILES - 1, first : first + GROUP], in_=v_acc_of[(LAST_TILE, c)][:])
+            copy = nc.vector.tensor_copy if 1 else nc.scalar.copy
+            copy(out=v_rows[:, BATCHES - 1, ROW_TILES - 1, first : first + GROUP], in_=v_acc_of[(LAST_TILE, c)][:])
             regroup_v(BATCHES - 1, first, GROUP)
             quantise_v(BATCHES - 1, first, GROUP)
 
@@ -272,7 +275,7 @@ def tile_multiheadlatentattention_pb_k_kernel(
                     )
             first = b * ROW_TILES + pair * STEP_TILES
             ctx_rows = out_pool.tile([P, STEP_TILES, GROUP_HEADS, HEAD_DIM], F32)
-            if c == 1 and pair == 1 and TAIL == 2:
+            if (c == 1 and pair == 1 and TAIL == 2) or (c == 0 and TAIL == 3) or (pair == 1 and TAIL == 4):
                 for a in range(STEP_TILES):
                     for h2 in range(GROUP_HEADS):
                         h = c * GROUP_HEADS + h2
@@ -465,6 +468,6 @@ def tile_multiheadlatentattention_pb_k_kernel(
             if TAIL and last in (2, 3):
                 for pair in range(STEPS_PER_HEAD):
                     context_half(last - 2, pair)
-            late = turn - ROUNDS_PER_BATCH - 4
+            late = turn - ROUNDS_PER_BATCH - 3
             if late >= 0 and (not TAIL or turn < ROUNDS) and late % ROUNDS_PER_BATCH < ROW_TILES:
                 context(late // ROUNDS_PER_BATCH, late % ROUNDS_PER_BATCH)

from contextlib import ExitStack
import math

import concourse.mybir as mybir
from concourse.masks import make_identity

F32 = mybir.dt.float32
BF16 = mybir.dt.bfloat16
I32 = mybir.dt.int32
U32 = mybir.dt.uint32
U8 = mybir.dt.uint8
FP8X4 = mybir.dt.float8_e4m3fn_x4

P = 128
PACK = 4
K_PASS = P * PACK

BATCHES = 2
TOKENS = 512
HEADS = 4
HEAD_DIM = 128
LATENT = 8192
V_WIDTH = HEADS * HEAD_DIM

PASSES = LATENT // K_PASS
ROW_TILES = TOKENS // P
ROUND_PASSES = 8
ROUND_BANKS = ROUND_PASSES // 2
ROUNDS_PER_TILE = PASSES // ROUND_PASSES
ROUNDS_PER_BATCH = ROW_TILES * ROUNDS_PER_TILE
ROUNDS = BATCHES * ROUNDS_PER_BATCH
ROUND_K = ROUND_PASSES * K_PASS
WORDS_PER_PASS = K_PASS // 2

STEP_TILES = 2
STEPS_PER_HEAD = ROW_TILES // STEP_TILES
STEPS = BATCHES * HEADS * STEPS_PER_HEAD

CV_LEAD = 2
ATTENTION_LEAD = 1
LOAD_ROUNDS = 1
LOADS = ROUNDS // LOAD_ROUNDS
CV_RAW_BUFS = 6
TAIL = 3
LAST_TILE = BATCHES * ROW_TILES - 1
GROUP_HEADS = 2
GROUPS = HEADS // GROUP_HEADS
GROUP = GROUP_HEADS * HEAD_DIM
VBANK = "0"
EC = "v"

SOFTMAX_SCALE = 1.0 / math.sqrt(HEAD_DIM)

FLOPS = 2 * BATCHES * TOKENS * LATENT * V_WIDTH + 2 * 2 * BATCHES * HEADS * TOKENS * TOKENS * HEAD_DIM


def tile_multiheadlatentattention_pb_k_kernel(
    tc, q_rot, k_rot, c_v, W_v_dec_words, W_v_dec_scales, out
):
    nc = tc.nc
    with ExitStack() as stack:
        keep = stack.enter_context(tc.tile_pool(name="keep", bufs=1))
        raw_pool = stack.enter_context(tc.tile_pool(name="raw", bufs=CV_RAW_BUFS))
        grouped_pool = stack.enter_context(tc.tile_pool(name="grouped", bufs=2))
        codes_pool = stack.enter_context(tc.tile_pool(name="codes", bufs=CV_LEAD + 2))
        soft_pool = stack.enter_context(tc.tile_pool(name="soft", bufs=3))
        small_pool = stack.enter_context(tc.tile_pool(name="small", bufs=3))
        out_pool = stack.enter_context(tc.tile_pool(name="result", bufs=6))
        work_psum = stack.enter_context(tc.psum_pool(name="work", bufs=4))
        score_psum = stack.enter_context(tc.psum_pool(name="score", bufs=STEP_TILES))
        v_psum = stack.enter_context(tc.psum_pool(name="v", bufs=2))
        stack.enter_context(tc.manual_schedule())

        ident_f32 = keep.tile([P, P], F32)
        ident_bf16 = keep.tile([P, P], BF16)
        w_words = keep.tile([P, PASSES, PACK * V_WIDTH], U8, align_bytes=64)
        w_scales = keep.tile([P, PASSES, V_WIDTH], U8, align_bytes=64)
        q_rows = keep.tile([P, BATCHES, ROW_TILES, V_WIDTH], BF16)
        k_rows = keep.tile([P, BATCHES, ROW_TILES, V_WIDTH], BF16)
        qk_t = keep.tile([P, BATCHES * HEADS, 2, TOKENS], BF16)
        e_codes = keep.tile([P, STEPS, STEP_TILES * P], U32, align_bytes=64)
        e_scales = keep.tile([P, STEPS, STEP_TILES * P], U8, align_bytes=64)
        row_sums = keep.tile([P, BATCHES * ROW_TILES, HEADS], F32)
        inverse_sums = keep.tile([P, BATCHES * ROW_TILES, HEADS], F32)
        v_rows = keep.tile([P, BATCHES, ROW_TILES, V_WIDTH], BF16)
        v_grouped = keep.tile([P, BATCHES, V_WIDTH, PACK], BF16, align_bytes=64)
        v_codes = keep.tile([P, BATCHES, V_WIDTH], U32, align_bytes=64)
        v_scales = keep.tile([P, BATCHES, V_WIDTH], U8, align_bytes=64)

        cv_raw_of = {}
        grouped_of = {}
        cv_codes_of = {}
        v_acc_of = {}
        peak_of = {}
        score_of = {}
        shift_of = {}
        e_rows_of = {}
        e_grouped_of = {}

        cv_tiles = c_v.rearrange("b (u p e) k -> b u e p k", u=2, e=2)

        def load_qk(b):
            nc.sync.dma_start(out=q_rows[:, b], in_=q_rot[b].rearrange("(i p) h d -> p i (h d)", p=P))
            nc.sync.dma_start(out=k_rows[:, b], in_=k_rot[b].rearrange("(i p) h d -> p i (h d)", p=P))

        def load_cv(n, parts=1):
            if not 0 <= n < LOADS:
                return
            row_tile, part = divmod(n, LOADS // (BATCHES * ROW_TILES))
            b, j = divmod(row_tile, ROW_TILES)
            u, e = divmod(j, 2)
            cv_raw = raw_pool.tile([P, LOAD_ROUNDS * ROUND_K], BF16)
            width = LOAD_ROUNDS * ROUND_K // parts
            for h in range(parts):
                first = part * LOAD_ROUNDS * ROUND_K + h * width
                nc.sync.dma_start(
                    out=cv_raw[:, h * width : (h + 1) * width], in_=cv_tiles[b, u, e, :, first : first + width]
                )
            cv_raw_of[n] = cv_raw

        def load_w_scales():
            for quadrant in range(4):
                nc.sync.dma_start(
                    out=w_scales[32 * quadrant : 32 * quadrant + 4].bitcast(I32),
                    in_=W_v_dec_scales[:, 4 * quadrant : 4 * quadrant + 4, :]
                    .rearrange("g r n -> r g n")
                    .bitcast(I32),
                )

        def load_w_words(first_pass, n_passes):
            passes = slice(first_pass, first_pass + n_passes)
            nc.sync.dma_start(
                out=w_words[:, passes, :].bitcast(I32),
                in_=W_v_dec_words[passes].rearrange("g p n t -> p g (n t)").bitcast(I32),
            )

        def raw_words(i):
            n, h = divmod(i, LOAD_ROUNDS)
            return cv_raw_of[n][:, h * ROUND_K : (h + 1) * ROUND_K].bitcast(F32)

        def transpose_cv(i, first_bank, last_bank):
            if not 0 <= i < ROUNDS:
                return
            if first_bank == 0:
                grouped = grouped_pool.tile([P, ROUND_PASSES, P, PACK], BF16, align_bytes=64)
                grouped_of[i] = grouped
            grouped = grouped_of[i]
            for c in range(first_bank, last_bank):
                bank = work_psum.tile([P, 2, 2, P], F32, tag="work")
                for g in range(2):
                    first = (2 * c + g) * WORDS_PER_PASS
                    for u in range(2):
                        nc.tensor.transpose(
                            bank[:, g, u, :], raw_words(i)[:, first + u : first + WORDS_PER_PASS : 2], ident_f32[:]
                        )
                copy = nc.vector.tensor_copy if VBANK[c % len(VBANK)] == "1" else nc.scalar.copy
                copy(out=grouped[:, 2 * c : 2 * c + 2].bitcast(F32), in_=bank[:].rearrange("p g u t -> p g t u"))

        def quantise_cv(i, half=None):
            if not 0 <= i < ROUNDS:
                return
            if half in (None, 0):
                cv_codes = codes_pool.tile([P, ROUND_PASSES * P], U32, align_bytes=64)
                cv_scales = codes_pool.tile([P, ROUND_PASSES * P], U8, align_bytes=64)
                cv_codes_of[i] = (cv_codes, cv_scales)
            cv_codes, cv_scales = cv_codes_of[i]
            passes = slice(0, ROUND_PASSES) if half is None else slice(half * ROUND_PASSES // 2, (half + 1) * ROUND_PASSES // 2)
            cols = slice(passes.start * P, passes.stop * P)
            nc.vector.quantize_mx(
                out=cv_codes[:, cols].bitcast(FP8X4),
                scales=cv_scales[:, cols],
                in_=grouped_of[i][:, passes].rearrange("p g t j -> p (g t j)"),
            )

        def project(i):
            row_tile, part = divmod(i, ROUNDS_PER_TILE)
            if not 0 <= i < ROUNDS or (TAIL and row_tile == LAST_TILE):
                return
            if part == 0:
                v_acc = v_psum.tile([P, V_WIDTH], F32)
                v_acc_of[row_tile] = v_acc
            v_acc = v_acc_of[row_tile]
            cv_codes, cv_scales = cv_codes_of[i]
            for g in range(ROUND_PASSES):
                k_pass = part * ROUND_PASSES + g
                tokens = slice(g * P, (g + 1) * P)
                nc.tensor.matmul_mx(
                    out=v_acc[:],
                    lhsT=cv_codes[:, tokens].bitcast(FP8X4),
                    lhsT_scale=cv_scales[:, tokens],
                    rhs=w_words[:, k_pass, :].bitcast(FP8X4),
                    rhs_scale=w_scales[:, k_pass, :],
                    start=(k_pass == 0),
                    stop=(k_pass == PASSES - 1),
                )

        def project_half(part, c):
            if part == 0:
                v_acc = v_psum.tile([P, GROUP], F32)
                v_acc_of[(LAST_TILE, c)] = v_acc
            v_acc = v_acc_of[(LAST_TILE, c)]
            cols = slice(c * GROUP, (c + 1) * GROUP)
            cv_codes, cv_scales = cv_codes_of[LAST_TILE * ROUNDS_PER_TILE + part]
            for g in range(ROUND_PASSES):
                k_pass = part * ROUND_PASSES + g
                tokens = slice(g * P, (g + 1) * P)
                nc.tensor.matmul_mx(
                    out=v_acc[:],
                    lhsT=cv_codes[:, tokens].bitcast(FP8X4),
                    lhsT_scale=cv_scales[:, tokens],
                    rhs=w_words[:, k_pass, PACK * c * GROUP : PACK * (c + 1) * GROUP].bitcast(FP8X4),
                    rhs_scale=w_scales[:, k_pass, cols],
                    start=(k_pass == 0),
                    stop=(k_pass == PASSES - 1),
                )

        def regroup_v(b, first, width):
            cols = slice(first, first + width)
            nc.vector.tensor_copy(out=v_grouped[:, b, cols, :], in_=v_rows[:, b, :, cols].rearrange("p j n -> p n j"))

        def quantise_v(b, first, width):
            cols = slice(first, first + width)
            nc.vector.quantize_mx(
                out=v_codes[:, b, cols].bitcast(FP8X4),
                scales=v_scales[:, b, cols],
                in_=v_grouped[:, b, cols, :].rearrange("p n j -> p (n j)"),
            )

        def hand_on_v(i):
            row_tile, part = divmod(i, ROUNDS_PER_TILE)
            if not 0 <= i < ROUNDS or part < ROUNDS_PER_TILE - 1 or (TAIL and row_tile == LAST_TILE):
                return
            b, j = divmod(row_tile, ROW_TILES)
            nc.scalar.copy(out=v_rows[:, b, j, :], in_=v_acc_of[row_tile][:])
            if j == ROW_TILES - 1 and not (TAIL and b == 0):
                regroup_v(b, 0, V_WIDTH)
                quantise_v(b, 0, V_WIDTH)

        def spread_v(turn):
            n = turn - ROUNDS_PER_BATCH
            if not TAIL:
                return
            if 0 <= n - 1 < GROUPS:
                for h in range((n - 1) * GROUP_HEADS, n * GROUP_HEADS):
                    quantise_v(0, h * HEAD_DIM, HEAD_DIM)
            if 0 <= n < GROUPS:
                for h in range(n * GROUP_HEADS, (n + 1) * GROUP_HEADS):
                    regroup_v(0, h * HEAD_DIM, HEAD_DIM)

        def hand_on_half(c):
            first = c * GROUP
            copy = nc.vector.tensor_copy if 1 else nc.scalar.copy
            copy(out=v_rows[:, BATCHES - 1, ROW_TILES - 1, first : first + GROUP], in_=v_acc_of[(LAST_TILE, c)][:])
            regroup_v(BATCHES - 1, first, GROUP)
            quantise_v(BATCHES - 1, first, GROUP)

        def context_half(c, pair):
            b = BATCHES - 1
            heads = slice(c * GROUP_HEADS, (c + 1) * GROUP_HEADS)
            ctx_bank = work_psum.tile([P, STEP_TILES, GROUP_HEADS, HEAD_DIM], F32, tag="work")
            for h2 in range(GROUP_HEADS):
                h = c * GROUP_HEADS + h2
                step = (b * HEADS + h) * STEPS_PER_HEAD + pair
                cols = slice(h * HEAD_DIM, (h + 1) * HEAD_DIM)
                for a in range(STEP_TILES):
                    queries = slice(a * P, (a + 1) * P)
                    nc.tensor.matmul_mx(
                        out=ctx_bank[:, a, h2, :],
                        lhsT=e_codes[:, step, queries].bitcast(FP8X4),
                        lhsT_scale=e_scales[:, step, queries],
                        rhs=v_codes[:, b, cols].bitcast(FP8X4),
                        rhs_scale=v_scales[:, b, cols],
                        start=True,
                        stop=True,
                    )
            first = b * ROW_TILES + pair * STEP_TILES
            ctx_rows = out_pool.tile([P, STEP_TILES, GROUP_HEADS, HEAD_DIM], F32)
            if (c == 1 and pair == 1 and TAIL == 2) or (c == 0 and TAIL == 3) or (pair == 1 and TAIL == 4):
                for a in range(STEP_TILES):
                    for h2 in range(GROUP_HEADS):
                        h = c * GROUP_HEADS + h2
                        nc.scalar.activation(
                            out=ctx_rows[:, a, h2, :],
                            in_=ctx_bank[:, a, h2, :],
                            func=mybir.ActivationFunctionType.Copy,
                            scale=inverse_sums[:, first + a, h : h + 1],
                        )
            else:
                inverse = inverse_sums[:, first : first + STEP_TILES, heads]
                nc.vector.tensor_tensor(
                    out=ctx_rows[:],
                    in0=ctx_bank[:],
                    in1=inverse.unsqueeze(3).to_broadcast([P, STEP_TILES, GROUP_HEADS, HEAD_DIM]),
                    op=mybir.AluOpType.mult,
                )
            rows = out[b, pair * STEP_TILES * P : (pair + 1) * STEP_TILES * P, c * GROUP : (c + 1) * GROUP]
            nc.sync.dma_start(
                out=rows.rearrange("(a p) d -> p a d", p=P), in_=ctx_rows[:].rearrange("p a h d -> p a (h d)")
            )

        def transpose_qk(head_block):
            if not 0 <= head_block < BATCHES * HEADS:
                return
            b, h = divmod(head_block, HEADS)
            qk_bank = work_psum.tile([P, 2, TOKENS], BF16, tag="work")
            for side, rows in enumerate((q_rows, k_rows)):
                for i in range(ROW_TILES):
                    nc.tensor.transpose(
                        qk_bank[:, side, i * P : (i + 1) * P], rows[:, b, i, h * P : (h + 1) * P], ident_bf16[:]
                    )
            nc.scalar.copy(out=qk_t[:, head_block], in_=qk_bank[:])

        def scores(step, a):
            if not 0 <= step < STEPS:
                return
            head_block, pair = divmod(step, STEPS_PER_HEAD)
            i = pair * STEP_TILES + a
            score = score_psum.tile([P, TOKENS], F32)
            nc.tensor.matmul(
                out=score[:],
                lhsT=qk_t[:, head_block, 0, i * P : (i + 1) * P],
                rhs=qk_t[:, head_block, 1, :],
                start=True,
                stop=True,
            )
            score_of[(step, a)] = score

        def maxima(step, a):
            if not 0 <= step < STEPS:
                return
            peak = small_pool.tile([P, 1], F32)
            nc.vector.tensor_reduce(
                out=peak[:], in_=score_of[(step, a)][:], axis=mybir.AxisListType.X, op=mybir.AluOpType.max
            )
            peak_of[(step, a)] = peak

        def shifts(step, a):
            if not 0 <= step < STEPS:
                return
            shift = small_pool.tile([P, 1], F32)
            nc.vector.tensor_scalar_mul(out=shift[:], in0=peak_of[(step, a)][:], scalar1=-SOFTMAX_SCALE)
            shift_of[(step, a)] = shift

        def exponentials(step, a):
            if not 0 <= step < STEPS:
                return
            head_block, pair = divmod(step, STEPS_PER_HEAD)
            b, h = divmod(head_block, HEADS)
            if a == 0:
                e_rows = soft_pool.tile([P, STEP_TILES, TOKENS], BF16)
                e_rows_of[step] = e_rows
            i = pair * STEP_TILES + a
            nc.scalar.activation(
                out=e_rows_of[step][:, a, :],
                in_=score_of[(step, a)][:],
                func=mybir.ActivationFunctionType.Exp,
                bias=shift_of[(step, a)][:],
                scale=SOFTMAX_SCALE,
                accum_out=row_sums[:, b * ROW_TILES + i, h : h + 1],
            )

        def transpose_e(step):
            if not 0 <= step < STEPS:
                return
            e_bank = work_psum.tile([P, STEP_TILES, 2, P], F32, tag="work")
            for a in range(STEP_TILES):
                e_words = e_rows_of[step][:, a, :].bitcast(F32)
                for u in range(2):
                    nc.tensor.transpose(e_bank[:, a, u, :], e_words[:, u * P : (u + 1) * P], ident_f32[:])
            e_grouped = soft_pool.tile([P, STEP_TILES, P, PACK], BF16, align_bytes=64)
            copy = nc.vector.tensor_copy if EC[step % len(EC)] == "v" else nc.scalar.copy
            copy(out=e_grouped[:].bitcast(F32), in_=e_bank[:].rearrange("p a u q -> p a q u"))
            e_grouped_of[step] = e_grouped

        def quantise_e(step):
            if not 0 <= step < STEPS:
                return
            nc.vector.quantize_mx(
                out=e_codes[:, step, :].bitcast(FP8X4),
                scales=e_scales[:, step, :],
                in_=e_grouped_of[step][:].rearrange("p a q j -> p (a q j)"),
            )
            b, step_in_batch = divmod(step, STEPS // BATCHES)
            if step_in_batch == STEPS // BATCHES - 1:
                tiles = slice(b * ROW_TILES, (b + 1) * ROW_TILES)
                nc.vector.reciprocal(out=inverse_sums[:, tiles, :], in_=row_sums[:, tiles, :])

        def context(b, i):
            pair, a = divmod(i, STEP_TILES)
            queries = slice(a * P, (a + 1) * P)
            ctx_bank = work_psum.tile([P, HEADS, HEAD_DIM], F32, tag="work")
            for h in range(HEADS):
                step = (b * HEADS + h) * STEPS_PER_HEAD + pair
                cols = slice(h * HEAD_DIM, (h + 1) * HEAD_DIM)
                nc.tensor.matmul_mx(
                    out=ctx_bank[:, h, :],
                    lhsT=e_codes[:, step, queries].bitcast(FP8X4),
                    lhsT_scale=e_scales[:, step, queries],
                    rhs=v_codes[:, b, cols].bitcast(FP8X4),
                    rhs_scale=v_scales[:, b, cols],
                    start=True,
                    stop=True,
                )
            inverse = inverse_sums[:, b * ROW_TILES + i, :]
            ctx_rows = out_pool.tile([P, HEADS, HEAD_DIM], F32)
            nc.vector.tensor_tensor(
                out=ctx_rows[:],
                in0=ctx_bank[:],
                in1=inverse.unsqueeze(2).to_broadcast([P, HEADS, HEAD_DIM]),
                op=mybir.AluOpType.mult,
            )
            nc.sync.dma_start(out=out[b, i * P : (i + 1) * P, :], in_=ctx_rows[:].rearrange("p h d -> p (h d)"))

        warm = small_pool.tile([P, 1], F32)
        nc.vector.memset(warm[:], 0.0)
        nc.scalar.activation(out=warm[:], in_=warm[:], func=mybir.ActivationFunctionType.Exp)
        make_identity(nc, ident_bf16[:])
        make_identity(nc, ident_f32[:])
        nc.vector.memset(w_scales[:].rearrange("p g n -> p (g n)").bitcast(I32), 0)
        load_qk(0)
        loaded = 0
        for c in "ccc0s1c23cq":
            if c == "q":
                load_qk(1)
            elif c == "s":
                load_w_scales()
            elif c == "c":
                load_cv(loaded, 2 if loaded == 0 else 1)
                loaded += 1
            else:
                load_w_words(4 * int(c), 4)
        for n in range(loaded, CV_RAW_BUFS):
            load_cv(n)

        halves_at = {0: ((0, 0),), 1: ((1, 0), (0, 1), (1, 1))}
        first_turn = -max(ATTENTION_LEAD + 3, CV_LEAD + 1)
        for turn in range(first_turn, ROUNDS + ROW_TILES):
            step = turn + ATTENTION_LEAD
            cv = turn + CV_LEAD
            freed = turn + CV_LEAD
            if freed > 0 and freed % LOAD_ROUNDS == 0:
                load_cv(freed // LOAD_ROUNDS - 1 + CV_RAW_BUFS)
            transpose_e(step - 1)
            transpose_cv(cv, 0, 2)
            scores(step + 1, 0)
            quantise_e(step - 1)
            maxima(step + 1, 0)
            transpose_cv(cv, 2, 4)
            if step % STEPS_PER_HEAD == 0:
                transpose_qk(step // STEPS_PER_HEAD + 1)
            scores(step + 1, 1)
            quantise_cv(cv, 0)
            shifts(step + 1, 0)
            exponentials(step + 1, 0)
            maxima(step + 1, 1)
            quantise_cv(cv, 1)
            shifts(step + 1, 1)
            exponentials(step + 1, 1)
            project(turn)
            hand_on_v(turn)
            spread_v(turn)
            last = turn - LAST_TILE * ROUNDS_PER_TILE
            if TAIL and last in halves_at:
                for part, c in halves_at[last]:
                    project_half(part, c)
                    if part == ROUNDS_PER_TILE - 1:
                        hand_on_half(c)
            if TAIL and last in (2, 3):
                for pair in range(STEPS_PER_HEAD):
                    context_half(last - 2, pair)
            late = turn - ROUNDS_PER_BATCH - 3
            if late >= 0 and (not TAIL or turn < ROUNDS) and late % ROUNDS_PER_BATCH < ROW_TILES:
                context(late // ROUNDS_PER_BATCH, late % ROUNDS_PER_BATCH)
